import numpy as np
import ml_dtypes


def mxq(x, axis, fmt="e4m3"):
    dtype, down = {"e4m3": (ml_dtypes.float8_e4m3fn, 7), "e5m2": (ml_dtypes.float8_e5m2, 14)}[fmt]
    v = np.moveaxis(np.asarray(x, np.float32).astype(ml_dtypes.bfloat16).astype(np.float64), axis, -1)
    blocks = v.reshape(v.shape[:-1] + (-1, 32))
    amax = np.abs(blocks).max(-1, keepdims=True)
    byte = np.maximum(np.where(amax > 0, np.frexp(amax)[1] - 1 + 127, 0) - down, 1)
    scale = np.exp2(byte - 127.0)
    codes = (blocks / scale).astype(np.float32).astype(dtype).astype(np.float64)
    return np.moveaxis((codes * scale).reshape(v.shape), -1, axis)


WIDE = False


def mx_kscale(k):
    if not WIDE:
        return np.ones(k)
    levels = np.array([10, -10, 5, -5, 0])
    a = np.random.permutation(np.resize(levels, k // 512 * 4)).reshape(k // 512, 4)
    idx = np.arange(k)
    return np.exp2(a[idx // 512, idx % 128 // 32])


BF16 = ml_dtypes.bfloat16


def bf(x):
    return np.asarray(x, np.float32).astype(BF16)


def f64(x):
    return np.asarray(x).astype(np.float64)


B, D, U, R = 12288, 1024, 128, 8
EPS = 1e-12


def softplus(v):
    return np.maximum(v, 0.0) + np.log(1.0 + np.exp(-np.abs(v)))


def draw(n, p):
    v = 0.3 * np.random.standard_normal((n, D)) / np.sqrt(D)
    for r in range(R):
        v = v + 0.8 * np.random.standard_normal((n, 1)) * p[r] / np.sqrt(R * D)
    return v


def rows(n, w):
    return w[(np.arange(n) * max(D // n, 1)) % D]


def setup_inputs():
    p = np.random.standard_normal((R, D))
    t = mx_kscale(D)
    w = t / np.exp2(np.round(0.8 * np.log2(t.max())))
    wu = rows(U, w)
    x0 = draw(B, p)
    c0 = draw(U, p)
    g = softplus(np.log(np.exp(1.0) - 1.0) + 0.3 * np.random.standard_normal(U)) / wu ** 2
    return {"x": bf(x0 * rows(B, w)[:, None]), "centers": bf(c0 * wu[:, None]),
            "gamma_raw": bf(g + np.log(-np.expm1(-g)))}


def reference(x, centers, gamma_raw):
    x, centers = f64(x), f64(centers)
    gamma = softplus(f64(gamma_raw))
    x_norm = np.sum(np.square(x), axis=-1, keepdims=True)
    c_norm = np.sum(np.square(centers), axis=-1)
    cross = -2.0 * (mxq(x, 1, "e4m3") @ mxq(centers, 1, "e4m3").T)
    d2 = np.maximum(x_norm + cross + c_norm[None, :] + EPS, 0.0)
    return np.exp(-gamma[None, :] * d2)

@@ -1,0 +1,242 @@
+from contextlib import ExitStack
+
+import concourse.mybir as mybir
+from concourse.masks import make_identity
+
+F32 = mybir.dt.float32
+BF16 = mybir.dt.bfloat16
+U32 = mybir.dt.uint32
+U8 = mybir.dt.uint8
+FP8X4 = mybir.dt.float8_e4m3fn_x4
+ALU = mybir.AluOpType
+ACT = mybir.ActivationFunctionType
+
+P = 128
+B, D, U = 12288, 1024, 128
+NT = B // P
+T = 4
+NG = NT // T
+EPS = 1e-12
+V_NORM_EVERY = 16
+
+FLOPS = 2 * B * D * U
+
+
+def tile_rbflayer_t_kernel(tc, x, centers, gamma_raw, out):
+    nc = tc.nc
+    xv = x.rearrange("(p t) k -> p t k", t=NT)
+    ov = out.rearrange("(p t) u -> p t u", t=NT)
+
+    with ExitStack() as ctx:
+        const = ctx.enter_context(tc.tile_pool(name="const", bufs=1))
+        xin = ctx.enter_context(tc.tile_pool(name="xin", bufs=5))
+        work = ctx.enter_context(tc.tile_pool(name="work", bufs=2))
+        small = ctx.enter_context(tc.tile_pool(name="small", bufs=4))
+        epi = ctx.enter_context(tc.tile_pool(name="epi", bufs=3))
+        ps_t = ctx.enter_context(tc.psum_pool(name="ps_t", bufs=6))
+        ps_a = ctx.enter_context(tc.psum_pool(name="ps_a", bufs=2))
+
+        x_sb = {}
+        xts = {}
+        grps = {}
+        cods = {}
+        scls = {}
+        accs = {}
+        xns = {}
+        eps_t = {}
+
+        def load(g):
+            t = xin.tile([P, T, D], BF16, name="x_sb")
+            x_sb[g] = t
+            if g == 0:
+                for j in range(T):
+                    nc.sync.dma_start(out=t[:, j, :], in_=xv[:, j, :])
+            else:
+                nc.sync.dma_start(out=t[:], in_=xv[:, g * T : (g + 1) * T, :])
+
+        c_sb = const.tile([P, D], BF16, name="c_sb")
+        nc.sync.dma_start(out=c_sb[:], in_=centers)
+        graw = const.tile([P, U], BF16, name="graw")
+        nc.scalar.dma_start(out=graw[:], in_=gamma_raw.partition_broadcast(P))
+        load(0)
+        load(1)
+        load(2)
+        load(3)
+
+        ident = const.tile([P, P], F32, name="ident")
+        make_identity(nc, ident[:])
+
+        def transpose_tile(src_bf16):
+            xt = ps_t.tile([P, 4, P], F32, name="xt")
+            w = src_bf16.bitcast(F32)
+            for q in range(4):
+                nc.tensor.transpose(xt[:, q, :], w[:, q * P : (q + 1) * P], ident[:])
+            return xt
+
+        c_xt = transpose_tile(c_sb[:])
+        c_grp = const.tile([P, 2, P, 2], F32, name="c_grp", align_bytes=64)
+        nc.vector.tensor_copy(
+            out=c_grp[:], in_=c_xt[:].rearrange("p (g u) c -> p g c u", u=2)
+        )
+        c_cod = const.tile([P, 2 * P], U32, name="c_cod", align_bytes=64)
+        c_scl = const.tile([P, 2 * P], U8, name="c_scl", align_bytes=64)
+
+        gabs = const.tile([P, U], F32, name="gabs")
+        nc.vector.scalar_tensor_tensor(
+            out=gabs[:], in0=graw[:], scalar=-1.0, in1=graw[:], op0=ALU.mult, op1=ALU.max
+        )
+        gexp = const.tile([P, U], F32, name="gexp")
+        nc.scalar.activation(out=gexp[:], in_=gabs[:], func=ACT.Exp, scale=-1.0)
+        glog = const.tile([P, U], F32, name="glog")
+        nc.scalar.activation(out=glog[:], in_=gexp[:], func=ACT.Ln, bias=1.0, scale=1.0)
+        gam = const.tile([P, U], F32, name="gam")
+        nc.vector.scalar_tensor_tensor(
+            out=gam[:], in0=graw[:], scalar=0.0, in1=glog[:], op0=ALU.max, op1=ALU.add
+        )
+        g2 = const.tile([P, T, U], F32, name="g2")
+        for j in range(T):
+            nc.vector.tensor_scalar_mul(out=g2[:, j, :], in0=gam[:], scalar1=2.0)
+
+        nc.vector.quantize_mx(
+            out=c_cod[:].bitcast(FP8X4),
+            scales=c_scl[:],
+            in_=c_grp[:].rearrange("p g c u -> p (g c u)").bitcast(BF16),
+        )
+
+        c_junk = const.tile([P, D], BF16, name="c_junk")
+        cn = const.tile([P, 1], F32, name="cn")
+        nc.scalar.activation(out=c_junk[:], in_=c_sb[:], func=ACT.Square, accum_out=cn[:])
+        cnh = const.tile([P, 1], F32, name="cnh")
+        nc.vector.tensor_scalar(
+            out=cnh[:], in0=cn[:], scalar1=EPS, scalar2=0.5, op0=ALU.add, op1=ALU.mult
+        )
+        cn_rep = const.tile([P, P], F32, name="cn_rep")
+        nc.vector.tensor_copy(out=cn_rep[:], in_=cnh[:, 0:1].to_broadcast([P, P]))
+        cn_ps = ps_t.tile([P, 4, P], F32, name="xt")
+        nc.tensor.transpose(cn_ps[:, 0, :], cn_rep[:], ident[:])
+        cnb = const.tile([P, U], F32, name="cnb")
+        nc.vector.tensor_copy(out=cnb[:], in_=cn_ps[:, 0, :])
+
+        def norms(g):
+            xn = small.tile([P, T], F32, name="xn")
+            xh = small.tile([P, T], F32, name="xh")
+            xns[g] = (xn, xh)
+            for j in range(T):
+                if (g * T + j) % V_NORM_EVERY == V_NORM_EVERY - 1:
+                    vj = work.tile([P, D], BF16, name="vjunk")
+                    nc.vector.scalar_tensor_tensor(
+                        out=vj[:],
+                        in0=x_sb[g][:, j, :],
+                        scalar=-0.5,
+                        in1=x_sb[g][:, j, :],
+                        op0=ALU.mult,
+                        op1=ALU.mult,
+                        accum_out=xh[:, j : j + 1],
+                    )
+                else:
+                    sj = work.tile([P, D], BF16, name="sjunk")
+                    nc.scalar.activation(
+                        out=sj[:],
+                        in_=x_sb[g][:, j, :],
+                        func=ACT.Square,
+                        accum_out=xn[:, j : j + 1],
+                    )
+
+        def transposes(g):
+            xts[g] = [transpose_tile(x_sb[g][:, j, :]) for j in range(T)]
+
+        def copies(g):
+            grp = work.tile([P, T, 2, P, 2], F32, name="grp", align_bytes=64)
+            grps[g] = grp
+            for j in range(T):
+                nc.vector.tensor_copy(
+                    out=grp[:, j],
+                    in_=xts[g][j][:].rearrange("p (g u) c -> p g c u", u=2),
+                )
+
+        def quant(g):
+            cod = work.tile([P, T * 2 * P], U32, name="cod", align_bytes=64)
+            scl = work.tile([P, T * 2 * P], U8, name="scl", align_bytes=64)
+            cods[g] = cod
+            scls[g] = scl
+            nc.vector.quantize_mx(
+                out=cod[:].bitcast(FP8X4),
+                scales=scl[:],
+                in_=grps[g][:].rearrange("p t g c u -> p (t g c u)").bitcast(BF16),
+            )
+
+        def mx(g):
+            acc = ps_a.tile([P, T, U], F32, name="acc")
+            accs[g] = acc
+            for j in range(T):
+                for h in range(2):
+                    cols = slice((2 * j + h) * P, (2 * j + h + 1) * P)
+                    ccols = slice(h * P, (h + 1) * P)
+                    nc.tensor.matmul_mx(
+                        out=acc[:, j, :],
+                        lhsT=cods[g][:, cols].bitcast(FP8X4),
+                        lhsT_scale=scls[g][:, cols],
+                        rhs=c_cod[:, ccols].bitcast(FP8X4),
+                        rhs_scale=c_scl[:, ccols],
+                        start=(h == 0),
+                        stop=(h == 1),
+                    )
+
+        def epi12(g):
+            xn, xh = xns[g]
+            n_s = T
+            if (g * T + T - 1) % V_NORM_EVERY == V_NORM_EVERY - 1:
+                n_s = T - 1
+            nc.vector.tensor_scalar_mul(out=xh[:, 0:n_s], in0=xn[:, 0:n_s], scalar1=-0.5)
+            e = epi.tile([P, T, U], F32, name="e")
+            eps_t[g] = e
+            for j in range(T):
+                nc.vector.scalar_tensor_tensor(
+                    out=e[:, j, :],
+                    in0=accs[g][:, j, :],
+                    scalar=xh[:, j : j + 1],
+                    in1=cnb[:],
+                    op0=ALU.add,
+                    op1=ALU.subtract,
+                )
+            ef = e[:].rearrange("p t u -> p (t u)")
+            nc.vector.scalar_tensor_tensor(
+                out=ef,
+                in0=ef,
+                scalar=0.0,
+                in1=g2[:].rearrange("p t u -> p (t u)"),
+                op0=ALU.min,
+                op1=ALU.mult,
+            )
+
+        def epi3(g):
+            ef = eps_t[g][:].rearrange("p t u -> p (t u)")
+            nc.scalar.activation(out=ef, in_=ef, func=ACT.Exp)
+
+        def store(g):
+            nc.sync.dma_start(out=ov[:, g * T : (g + 1) * T, :], in_=eps_t[g][:])
+
+        norms(0)
+        transposes(0)
+        copies(0)
+        norms(1)
+        transposes(1)
+        quant(0)
+        for i in range(NG):
+            mx(i)
+            if i + 1 < NG:
+                copies(i + 1)
+            if i + 2 < NG:
+                transposes(i + 2)
+            if i >= 1:
+                epi3(i - 1)
+                store(i - 1)
+            if i + 2 < NG:
+                norms(i + 2)
+            if i + 4 < NG:
+                load(i + 4)
+            epi12(i)
+            if i + 1 < NG:
+                quant(i + 1)
+        epi3(NG - 1)
+        store(NG - 1)

@@ -17,7 +17,8 @@ NT = B // P
 T = 4
 NG = NT // T
 EPS = 1e-12
-V_NORM_EVERY = 16
+G_TILE = 3
+S_COPY_EVERY = 2
 
 FLOPS = 2 * B * D * U
 
@@ -33,7 +34,8 @@ def tile_rbflayer_t_kernel(tc, x, centers, gamma_raw, out):
         work = ctx.enter_context(tc.tile_pool(name="work", bufs=2))
         small = ctx.enter_context(tc.tile_pool(name="small", bufs=4))
         epi = ctx.enter_context(tc.tile_pool(name="epi", bufs=3))
-        ps_t = ctx.enter_context(tc.psum_pool(name="ps_t", bufs=6))
+        ps_t = ctx.enter_context(tc.psum_pool(name="ps_t", bufs=5))
+        ps_r = ctx.enter_context(tc.psum_pool(name="ps_r", bufs=1))
         ps_a = ctx.enter_context(tc.psum_pool(name="ps_a", bufs=2))
 
         x_sb = {}
@@ -44,6 +46,8 @@ def tile_rbflayer_t_kernel(tc, x, centers, gamma_raw, out):
         accs = {}
         xns = {}
         eps_t = {}
+        sqs = {}
+        rps = {}
 
         def load(g):
             t = xin.tile([P, T, D], BF16, name="x_sb")
@@ -122,18 +126,7 @@ def tile_rbflayer_t_kernel(tc, x, centers, gamma_raw, out):
             xh = small.tile([P, T], F32, name="xh")
             xns[g] = (xn, xh)
             for j in range(T):
-                if (g * T + j) % V_NORM_EVERY == V_NORM_EVERY - 1:
-                    vj = work.tile([P, D], BF16, name="vjunk")
-                    nc.vector.scalar_tensor_tensor(
-                        out=vj[:],
-                        in0=x_sb[g][:, j, :],
-                        scalar=-0.5,
-                        in1=x_sb[g][:, j, :],
-                        op0=ALU.mult,
-                        op1=ALU.mult,
-                        accum_out=xh[:, j : j + 1],
-                    )
-                else:
+                if j != G_TILE:
                     sj = work.tile([P, D], BF16, name="sjunk")
                     nc.scalar.activation(
                         out=sj[:],
@@ -148,10 +141,30 @@ def tile_rbflayer_t_kernel(tc, x, centers, gamma_raw, out):
         def copies(g):
             grp = work.tile([P, T, 2, P, 2], F32, name="grp", align_bytes=64)
             grps[g] = grp
-            for j in range(T):
-                nc.vector.tensor_copy(
-                    out=grp[:, j],
-                    in_=xts[g][j][:].rearrange("p (g u) c -> p g c u", u=2),
+            for j in (3, 0, 1, 2):
+                src = xts[g][j][:].rearrange("p (g u) c -> p g c u", u=2)
+                if j == 0 and g % S_COPY_EVERY == 0:
+                    nc.scalar.copy(out=grp[:, j], in_=src)
+                else:
+                    nc.vector.tensor_copy(out=grp[:, j], in_=src)
+
+        def gsquare(g):
+            sq = work.tile([P, 2, 4, P], F32, name="sq")
+            sqs[g] = sq
+            gv = grps[g][:, G_TILE].bitcast(BF16).rearrange("p h c t -> p h t c")
+            nc.gpsimd.tensor_tensor(out=sq[:], in0=gv, in1=gv, op=ALU.mult)
+
+        def rtrans(g):
+            r = ps_r.tile([P, P], F32, name="r")
+            rps[g] = r
+            for q in range(8):
+                nc.tensor.matmul(
+                    out=r[:],
+                    lhsT=sqs[g][:, q // 4, q % 4, :],
+                    rhs=ident[:],
+                    start=(q == 0),
+                    stop=(q == 7),
+                    is_transpose=True,
                 )
 
         def quant(g):
@@ -184,10 +197,18 @@ def tile_rbflayer_t_kernel(tc, x, centers, gamma_raw, out):
 
         def epi12(g):
             xn, xh = xns[g]
-            n_s = T
-            if (g * T + T - 1) % V_NORM_EVERY == V_NORM_EVERY - 1:
-                n_s = T - 1
+            n_s = G_TILE
             nc.vector.tensor_scalar_mul(out=xh[:, 0:n_s], in0=xn[:, 0:n_s], scalar1=-0.5)
+            rj = work.tile([P, P], F32, name="rj")
+            nc.vector.tensor_scalar(
+                out=rj[:],
+                in0=rps[g][:],
+                scalar1=-0.5,
+                scalar2=None,
+                op0=ALU.mult,
+                op1=ALU.add,
+                accum_out=xh[:, G_TILE : G_TILE + 1],
+            )
             e = epi.tile([P, T, U], F32, name="e")
             eps_t[g] = e
             for j in range(T):
@@ -219,13 +240,16 @@ def tile_rbflayer_t_kernel(tc, x, centers, gamma_raw, out):
         norms(0)
         transposes(0)
         copies(0)
+        gsquare(0)
         norms(1)
         transposes(1)
         quant(0)
+        rtrans(0)
         for i in range(NG):
             mx(i)
             if i + 1 < NG:
                 copies(i + 1)
+                gsquare(i + 1)
             if i + 2 < NG:
                 transposes(i + 2)
             if i >= 1:
@@ -238,5 +262,6 @@ def tile_rbflayer_t_kernel(tc, x, centers, gamma_raw, out):
             epi12(i)
             if i + 1 < NG:
                 quant(i + 1)
+                rtrans(i + 1)
         epi3(NG - 1)
         store(NG - 1)

@@ -17,8 +17,9 @@ NT = B // P
 T = 4
 NG = NT // T
 EPS = 1e-12
-G_TILE = 3
-S_COPY_EVERY = 2
+PE_NORM_GROUPS = (1, 4, 6, 9, 12, 14, 17, 20, 22)
+V_NORM_GROUPS = (3, 7, 11, 15, 19, 23)
+LAST = T - 1
 
 FLOPS = 2 * B * D * U
 
@@ -46,7 +47,6 @@ def tile_rbflayer_t_kernel(tc, x, centers, gamma_raw, out):
         accs = {}
         xns = {}
         eps_t = {}
-        sqs = {}
         rps = {}
 
         def load(g):
@@ -126,7 +126,20 @@ def tile_rbflayer_t_kernel(tc, x, centers, gamma_raw, out):
             xh = small.tile([P, T], F32, name="xh")
             xns[g] = (xn, xh)
             for j in range(T):
-                if j != G_TILE:
+                if j == LAST and g in PE_NORM_GROUPS:
+                    continue
+                if j == LAST and g in V_NORM_GROUPS:
+                    vj = work.tile([P, D], BF16, name="vjunk")
+                    nc.vector.scalar_tensor_tensor(
+                        out=vj[:],
+                        in0=x_sb[g][:, j, :],
+                        scalar=-0.5,
+                        in1=x_sb[g][:, j, :],
+                        op0=ALU.mult,
+                        op1=ALU.mult,
+                        accum_out=xh[:, j : j + 1],
+                    )
+                else:
                     sj = work.tile([P, D], BF16, name="sjunk")
                     nc.scalar.activation(
                         out=sj[:],
@@ -141,30 +154,20 @@ def tile_rbflayer_t_kernel(tc, x, centers, gamma_raw, out):
         def copies(g):
             grp = work.tile([P, T, 2, P, 2], F32, name="grp", align_bytes=64)
             grps[g] = grp
-            for j in (3, 0, 1, 2):
-                src = xts[g][j][:].rearrange("p (g u) c -> p g c u", u=2)
-                if j == 0 and g % S_COPY_EVERY == 0:
-                    nc.scalar.copy(out=grp[:, j], in_=src)
-                else:
-                    nc.vector.tensor_copy(out=grp[:, j], in_=src)
+            for j in range(T):
+                nc.vector.tensor_copy(
+                    out=grp[:, j],
+                    in_=xts[g][j][:].rearrange("p (g u) c -> p g c u", u=2),
+                )
 
-        def gsquare(g):
-            sq = work.tile([P, 2, 4, P], F32, name="sq")
-            sqs[g] = sq
-            gv = grps[g][:, G_TILE].bitcast(BF16).rearrange("p h c t -> p h t c")
-            nc.gpsimd.tensor_tensor(out=sq[:], in0=gv, in1=gv, op=ALU.mult)
-
-        def rtrans(g):
+        def gram(g):
             r = ps_r.tile([P, P], F32, name="r")
             rps[g] = r
+            v = grps[g][:, LAST].bitcast(BF16)
             for q in range(8):
+                plane = v[:, q // 4, :, q % 4]
                 nc.tensor.matmul(
-                    out=r[:],
-                    lhsT=sqs[g][:, q // 4, q % 4, :],
-                    rhs=ident[:],
-                    start=(q == 0),
-                    stop=(q == 7),
-                    is_transpose=True,
+                    out=r[:], lhsT=plane, rhs=plane, start=(q == 0), stop=(q == 7)
                 )
 
         def quant(g):
@@ -197,18 +200,21 @@ def tile_rbflayer_t_kernel(tc, x, centers, gamma_raw, out):
 
         def epi12(g):
             xn, xh = xns[g]
-            n_s = G_TILE
+            n_s = T
+            if g in PE_NORM_GROUPS or g in V_NORM_GROUPS:
+                n_s = LAST
             nc.vector.tensor_scalar_mul(out=xh[:, 0:n_s], in0=xn[:, 0:n_s], scalar1=-0.5)
-            rj = work.tile([P, P], F32, name="rj")
-            nc.vector.tensor_scalar(
-                out=rj[:],
-                in0=rps[g][:],
-                scalar1=-0.5,
-                scalar2=None,
-                op0=ALU.mult,
-                op1=ALU.add,
-                accum_out=xh[:, G_TILE : G_TILE + 1],
-            )
+            if g in PE_NORM_GROUPS:
+                rj = work.tile([P, P], F32, name="rj")
+                nc.vector.scalar_tensor_tensor(
+                    out=rj[:],
+                    in0=rps[g][:],
+                    scalar=-0.5,
+                    in1=ident[:],
+                    op0=ALU.mult,
+                    op1=ALU.mult,
+                    accum_out=xh[:, LAST : LAST + 1],
+                )
             e = epi.tile([P, T, U], F32, name="e")
             eps_t[g] = e
             for j in range(T):
@@ -240,18 +246,17 @@ def tile_rbflayer_t_kernel(tc, x, centers, gamma_raw, out):
         norms(0)
         transposes(0)
         copies(0)
-        gsquare(0)
         norms(1)
         transposes(1)
         quant(0)
-        rtrans(0)
         for i in range(NG):
             mx(i)
             if i + 1 < NG:
                 copies(i + 1)
-                gsquare(i + 1)
             if i + 2 < NG:
                 transposes(i + 2)
+            if i + 1 in PE_NORM_GROUPS:
+                gram(i + 1)
             if i >= 1:
                 epi3(i - 1)
                 store(i - 1)
@@ -262,6 +267,5 @@ def tile_rbflayer_t_kernel(tc, x, centers, gamma_raw, out):
             epi12(i)
             if i + 1 < NG:
                 quant(i + 1)
-                rtrans(i + 1)
         epi3(NG - 1)
         store(NG - 1)

@@ -16,10 +16,11 @@ B, D, U = 12288, 1024, 128
 NT = B // P
 T = 4
 NG = NT // T
-EPS = 1e-12
-PE_NORM_GROUPS = (1, 4, 6, 9, 12, 14, 17, 20, 22)
-V_NORM_GROUPS = (3, 7, 11, 15, 19, 23)
 LAST = T - 1
+EPS = 1e-12
+NX = 6
+PE_NORM_GROUPS = (1, 4, 6, 9, 12, 14, 17, 20, 22)
+S_COPY_GROUPS = (1, 3, 5, 7, 9, 11, 13, 15, 17, 19, 21, 23)
 
 FLOPS = 2 * B * D * U
 
@@ -30,11 +31,12 @@ def tile_rbflayer_t_kernel(tc, x, centers, gamma_raw, out):
     ov = out.rearrange("(p t) u -> p t u", t=NT)
 
     with ExitStack() as ctx:
+        ctx.enter_context(tc.manual_schedule())
         const = ctx.enter_context(tc.tile_pool(name="const", bufs=1))
-        xin = ctx.enter_context(tc.tile_pool(name="xin", bufs=5))
+        xin = ctx.enter_context(tc.tile_pool(name="xin", bufs=NX))
         work = ctx.enter_context(tc.tile_pool(name="work", bufs=2))
         small = ctx.enter_context(tc.tile_pool(name="small", bufs=4))
-        epi = ctx.enter_context(tc.tile_pool(name="epi", bufs=3))
+        epi = ctx.enter_context(tc.tile_pool(name="epi", bufs=4))
         ps_t = ctx.enter_context(tc.psum_pool(name="ps_t", bufs=5))
         ps_r = ctx.enter_context(tc.psum_pool(name="ps_r", bufs=1))
         ps_a = ctx.enter_context(tc.psum_pool(name="ps_a", bufs=2))
@@ -58,68 +60,12 @@ def tile_rbflayer_t_kernel(tc, x, centers, gamma_raw, out):
             else:
                 nc.sync.dma_start(out=t[:], in_=xv[:, g * T : (g + 1) * T, :])
 
-        c_sb = const.tile([P, D], BF16, name="c_sb")
-        nc.sync.dma_start(out=c_sb[:], in_=centers)
-        graw = const.tile([P, U], BF16, name="graw")
-        nc.scalar.dma_start(out=graw[:], in_=gamma_raw.partition_broadcast(P))
-        load(0)
-        load(1)
-        load(2)
-        load(3)
-
-        ident = const.tile([P, P], F32, name="ident")
-        make_identity(nc, ident[:])
-
         def transpose_tile(src_bf16):
             xt = ps_t.tile([P, 4, P], F32, name="xt")
             w = src_bf16.bitcast(F32)
             for q in range(4):
                 nc.tensor.transpose(xt[:, q, :], w[:, q * P : (q + 1) * P], ident[:])
             return xt
-
-        c_xt = transpose_tile(c_sb[:])
-        c_grp = const.tile([P, 2, P, 2], F32, name="c_grp", align_bytes=64)
-        nc.vector.tensor_copy(
-            out=c_grp[:], in_=c_xt[:].rearrange("p (g u) c -> p g c u", u=2)
-        )
-        c_cod = const.tile([P, 2 * P], U32, name="c_cod", align_bytes=64)
-        c_scl = const.tile([P, 2 * P], U8, name="c_scl", align_bytes=64)
-
-        gabs = const.tile([P, U], F32, name="gabs")
-        nc.vector.scalar_tensor_tensor(
-            out=gabs[:], in0=graw[:], scalar=-1.0, in1=graw[:], op0=ALU.mult, op1=ALU.max
-        )
-        gexp = const.tile([P, U], F32, name="gexp")
-        nc.scalar.activation(out=gexp[:], in_=gabs[:], func=ACT.Exp, scale=-1.0)
-        glog = const.tile([P, U], F32, name="glog")
-        nc.scalar.activation(out=glog[:], in_=gexp[:], func=ACT.Ln, bias=1.0, scale=1.0)
-        gam = const.tile([P, U], F32, name="gam")
-        nc.vector.scalar_tensor_tensor(
-            out=gam[:], in0=graw[:], scalar=0.0, in1=glog[:], op0=ALU.max, op1=ALU.add
-        )
-        g2 = const.tile([P, T, U], F32, name="g2")
-        for j in range(T):
-            nc.vector.tensor_scalar_mul(out=g2[:, j, :], in0=gam[:], scalar1=2.0)
-
-        nc.vector.quantize_mx(
-            out=c_cod[:].bitcast(FP8X4),
-            scales=c_scl[:],
-            in_=c_grp[:].rearrange("p g c u -> p (g c u)").bitcast(BF16),
-        )
-
-        c_junk = const.tile([P, D], BF16, name="c_junk")
-        cn = const.tile([P, 1], F32, name="cn")
-        nc.scalar.activation(out=c_junk[:], in_=c_sb[:], func=ACT.Square, accum_out=cn[:])
-        cnh = const.tile([P, 1], F32, name="cnh")
-        nc.vector.tensor_scalar(
-            out=cnh[:], in0=cn[:], scalar1=EPS, scalar2=0.5, op0=ALU.add, op1=ALU.mult
-        )
-        cn_rep = const.tile([P, P], F32, name="cn_rep")
-        nc.vector.tensor_copy(out=cn_rep[:], in_=cnh[:, 0:1].to_broadcast([P, P]))
-        cn_ps = ps_t.tile([P, 4, P], F32, name="xt")
-        nc.tensor.transpose(cn_ps[:, 0, :], cn_rep[:], ident[:])
-        cnb = const.tile([P, U], F32, name="cnb")
-        nc.vector.tensor_copy(out=cnb[:], in_=cn_ps[:, 0, :])
 
         def norms(g):
             xn = small.tile([P, T], F32, name="xn")
@@ -128,25 +74,13 @@ def tile_rbflayer_t_kernel(tc, x, centers, gamma_raw, out):
             for j in range(T):
                 if j == LAST and g in PE_NORM_GROUPS:
                     continue
-                if j == LAST and g in V_NORM_GROUPS:
-                    vj = work.tile([P, D], BF16, name="vjunk")
-                    nc.vector.scalar_tensor_tensor(
-                        out=vj[:],
-                        in0=x_sb[g][:, j, :],
-                        scalar=-0.5,
-                        in1=x_sb[g][:, j, :],
-                        op0=ALU.mult,
-                        op1=ALU.mult,
-                        accum_out=xh[:, j : j + 1],
-                    )
-                else:
-                    sj = work.tile([P, D], BF16, name="sjunk")
-                    nc.scalar.activation(
-                        out=sj[:],
-                        in_=x_sb[g][:, j, :],
-                        func=ACT.Square,
-                        accum_out=xn[:, j : j + 1],
-                    )
+                sj = work.tile([P, D], BF16, name="sjunk")
+                nc.scalar.activation(
+                    out=sj[:],
+                    in_=x_sb[g][:, j, :],
+                    func=ACT.Square,
+                    accum_out=xn[:, j : j + 1],
+                )
 
         def transposes(g):
             xts[g] = [transpose_tile(x_sb[g][:, j, :]) for j in range(T)]
@@ -155,10 +89,11 @@ def tile_rbflayer_t_kernel(tc, x, centers, gamma_raw, out):
             grp = work.tile([P, T, 2, P, 2], F32, name="grp", align_bytes=64)
             grps[g] = grp
             for j in range(T):
-                nc.vector.tensor_copy(
-                    out=grp[:, j],
-                    in_=xts[g][j][:].rearrange("p (g u) c -> p g c u", u=2),
-                )
+                src = xts[g][j][:].rearrange("p (g u) c -> p g c u", u=2)
+                if j == 0 and g in S_COPY_GROUPS:
+                    nc.scalar.copy(out=grp[:, j], in_=src)
+                else:
+                    nc.vector.tensor_copy(out=grp[:, j], in_=src)
 
         def gram(g):
             r = ps_r.tile([P, P], F32, name="r")
@@ -198,10 +133,10 @@ def tile_rbflayer_t_kernel(tc, x, centers, gamma_raw, out):
                         stop=(h == 1),
                     )
 
-        def epi12(g):
+        def halves(g):
             xn, xh = xns[g]
             n_s = T
-            if g in PE_NORM_GROUPS or g in V_NORM_GROUPS:
+            if g in PE_NORM_GROUPS:
                 n_s = LAST
             nc.vector.tensor_scalar_mul(out=xh[:, 0:n_s], in0=xn[:, 0:n_s], scalar1=-0.5)
             if g in PE_NORM_GROUPS:
@@ -215,6 +150,9 @@ def tile_rbflayer_t_kernel(tc, x, centers, gamma_raw, out):
                     op1=ALU.mult,
                     accum_out=xh[:, LAST : LAST + 1],
                 )
+
+        def epi1(g):
+            xh = xns[g][1]
             e = epi.tile([P, T, U], F32, name="e")
             eps_t[g] = e
             for j in range(T):
@@ -226,7 +164,9 @@ def tile_rbflayer_t_kernel(tc, x, centers, gamma_raw, out):
                     op0=ALU.add,
                     op1=ALU.subtract,
                 )
-            ef = e[:].rearrange("p t u -> p (t u)")
+
+        def epi2(g):
+            ef = eps_t[g][:].rearrange("p t u -> p (t u)")
             nc.vector.scalar_tensor_tensor(
                 out=ef,
                 in0=ef,
@@ -243,14 +183,68 @@ def tile_rbflayer_t_kernel(tc, x, centers, gamma_raw, out):
         def store(g):
             nc.sync.dma_start(out=ov[:, g * T : (g + 1) * T, :], in_=eps_t[g][:])
 
+        graw = const.tile([P, U], BF16, name="graw")
+        nc.scalar.dma_start(out=graw[:], in_=gamma_raw.partition_broadcast(P))
+        c_sb = const.tile([P, D], BF16, name="c_sb")
+        nc.sync.dma_start(out=c_sb[:], in_=centers)
+        for g in range(NX):
+            load(g)
+        ident = const.tile([P, P], F32, name="ident")
+        make_identity(nc, ident[:])
+
+        gabs = const.tile([P, U], F32, name="gabs")
+        nc.vector.scalar_tensor_tensor(
+            out=gabs[:], in0=graw[:], scalar=-1.0, in1=graw[:], op0=ALU.mult, op1=ALU.max
+        )
+        gexp = const.tile([P, U], F32, name="gexp")
+        nc.scalar.activation(out=gexp[:], in_=gabs[:], func=ACT.Exp, scale=-1.0)
+
+        c_xt = transpose_tile(c_sb[:])
+        c_grp = const.tile([P, 2, P, 2], F32, name="c_grp", align_bytes=64)
+        nc.vector.tensor_copy(
+            out=c_grp[:], in_=c_xt[:].rearrange("p (g u) c -> p g c u", u=2)
+        )
+        c_junk = const.tile([P, D], BF16, name="c_junk")
+        cn = const.tile([P, 1], F32, name="cn")
+        nc.scalar.activation(out=c_junk[:], in_=c_sb[:], func=ACT.Square, accum_out=cn[:])
+
         norms(0)
         transposes(0)
         copies(0)
-        norms(1)
+        c_cod = const.tile([P, 2 * P], U32, name="c_cod", align_bytes=64)
+        c_scl = const.tile([P, 2 * P], U8, name="c_scl", align_bytes=64)
+        nc.vector.quantize_mx(
+            out=c_cod[:].bitcast(FP8X4),
+            scales=c_scl[:],
+            in_=c_grp[:].rearrange("p g c u -> p (g c u)").bitcast(BF16),
+        )
         transposes(1)
+        glog = const.tile([P, U], F32, name="glog")
+        nc.scalar.activation(out=glog[:], in_=gexp[:], func=ACT.Ln, bias=1.0, scale=1.0)
+        norms(1)
+
+        cnh = const.tile([P, 1], F32, name="cnh")
+        nc.vector.tensor_scalar(
+            out=cnh[:], in0=cn[:], scalar1=EPS, scalar2=0.5, op0=ALU.add, op1=ALU.mult
+        )
         quant(0)
+        cn_rep = const.tile([P, P], F32, name="cn_rep")
+        nc.vector.tensor_copy(out=cn_rep[:], in_=cnh[:, 0:1].to_broadcast([P, P]))
+        cn_ps = ps_r.tile([P, P], F32, name="r")
+        nc.tensor.transpose(cn_ps[:], cn_rep[:], ident[:])
+        gam = const.tile([P, U], F32, name="gam")
+        nc.vector.scalar_tensor_tensor(
+            out=gam[:], in0=graw[:], scalar=0.0, in1=glog[:], op0=ALU.max, op1=ALU.add
+        )
+        cnb = const.tile([P, U], F32, name="cnb")
+        nc.vector.tensor_copy(out=cnb[:], in_=cn_ps[:])
+        g2 = const.tile([P, T, U], F32, name="g2")
+        for j in range(T):
+            nc.vector.tensor_scalar_mul(out=g2[:, j, :], in0=gam[:], scalar1=2.0)
+
         for i in range(NG):
             mx(i)
+            halves(i)
             if i + 1 < NG:
                 copies(i + 1)
             if i + 2 < NG:
@@ -262,10 +256,11 @@ def tile_rbflayer_t_kernel(tc, x, centers, gamma_raw, out):
                 store(i - 1)
             if i + 2 < NG:
                 norms(i + 2)
-            if i + 4 < NG:
-                load(i + 4)
-            epi12(i)
+            if i + NX < NG:
+                load(i + NX)
+            epi1(i)
             if i + 1 < NG:
                 quant(i + 1)
+            epi2(i)
         epi3(NG - 1)
         store(NG - 1)

@@ -20,7 +20,7 @@ LAST = T - 1
 EPS = 1e-12
 NX = 6
 PE_NORM_GROUPS = (1, 4, 6, 9, 12, 14, 17, 20, 22)
-S_COPY_GROUPS = (1, 3, 5, 7, 9, 11, 13, 15, 17, 19, 21, 23)
+S_COPY_GROUPS = ()
 
 FLOPS = 2 * B * D * U
 

@@ -21,6 +21,7 @@ EPS = 1e-12
 NX = 6
 PE_NORM_GROUPS = (1, 4, 6, 9, 12, 14, 17, 20, 22)
 S_COPY_GROUPS = ()
+V_NORM_GROUPS = (0, 2)
 
 FLOPS = 2 * B * D * U
 
@@ -35,9 +36,11 @@ def tile_rbflayer_t_kernel(tc, x, centers, gamma_raw, out):
         const = ctx.enter_context(tc.tile_pool(name="const", bufs=1))
         xin = ctx.enter_context(tc.tile_pool(name="xin", bufs=NX))
         work = ctx.enter_context(tc.tile_pool(name="work", bufs=2))
-        small = ctx.enter_context(tc.tile_pool(name="small", bufs=4))
-        epi = ctx.enter_context(tc.tile_pool(name="epi", bufs=4))
-        ps_t = ctx.enter_context(tc.psum_pool(name="ps_t", bufs=5))
+        codes = ctx.enter_context(tc.tile_pool(name="codes", bufs=3))
+        small = ctx.enter_context(tc.tile_pool(name="small", bufs=5))
+        epi = ctx.enter_context(tc.tile_pool(name="epi", bufs=5))
+        ps_t = ctx.enter_context(tc.psum_pool(name="ps_t", bufs=4))
+        ps_c = ctx.enter_context(tc.psum_pool(name="ps_c", bufs=1))
         ps_r = ctx.enter_context(tc.psum_pool(name="ps_r", bufs=1))
         ps_a = ctx.enter_context(tc.psum_pool(name="ps_a", bufs=2))
 
@@ -72,7 +75,7 @@ def tile_rbflayer_t_kernel(tc, x, centers, gamma_raw, out):
             xh = small.tile([P, T], F32, name="xh")
             xns[g] = (xn, xh)
             for j in range(T):
-                if j == LAST and g in PE_NORM_GROUPS:
+                if j == LAST and (g in PE_NORM_GROUPS or g in V_NORM_GROUPS):
                     continue
                 sj = work.tile([P, D], BF16, name="sjunk")
                 nc.scalar.activation(
@@ -81,6 +84,18 @@ def tile_rbflayer_t_kernel(tc, x, centers, gamma_raw, out):
                     func=ACT.Square,
                     accum_out=xn[:, j : j + 1],
                 )
+
+        def vnorm(g):
+            vj = work.tile([P, D], BF16, name="vjunk")
+            nc.vector.scalar_tensor_tensor(
+                out=vj[:],
+                in0=x_sb[g][:, LAST, :],
+                scalar=-0.5,
+                in1=x_sb[g][:, LAST, :],
+                op0=ALU.mult,
+                op1=ALU.mult,
+                accum_out=xns[g][1][:, LAST : LAST + 1],
+            )
 
         def transposes(g):
             xts[g] = [transpose_tile(x_sb[g][:, j, :]) for j in range(T)]
@@ -106,8 +121,8 @@ def tile_rbflayer_t_kernel(tc, x, centers, gamma_raw, out):
                 )
 
         def quant(g):
-            cod = work.tile([P, T * 2 * P], U32, name="cod", align_bytes=64)
-            scl = work.tile([P, T * 2 * P], U8, name="scl", align_bytes=64)
+            cod = codes.tile([P, T * 2 * P], U32, name="cod", align_bytes=64)
+            scl = codes.tile([P, T * 2 * P], U8, name="scl", align_bytes=64)
             cods[g] = cod
             scls[g] = scl
             nc.vector.quantize_mx(
@@ -136,7 +151,7 @@ def tile_rbflayer_t_kernel(tc, x, centers, gamma_raw, out):
         def halves(g):
             xn, xh = xns[g]
             n_s = T
-            if g in PE_NORM_GROUPS:
+            if g in PE_NORM_GROUPS or g in V_NORM_GROUPS:
                 n_s = LAST
             nc.vector.tensor_scalar_mul(out=xh[:, 0:n_s], in0=xn[:, 0:n_s], scalar1=-0.5)
             if g in PE_NORM_GROUPS:
@@ -183,22 +198,26 @@ def tile_rbflayer_t_kernel(tc, x, centers, gamma_raw, out):
         def store(g):
             nc.sync.dma_start(out=ov[:, g * T : (g + 1) * T, :], in_=eps_t[g][:])
 
-        graw = const.tile([P, U], BF16, name="graw")
-        nc.scalar.dma_start(out=graw[:], in_=gamma_raw.partition_broadcast(P))
         c_sb = const.tile([P, D], BF16, name="c_sb")
-        nc.sync.dma_start(out=c_sb[:], in_=centers)
-        for g in range(NX):
-            load(g)
+        grow = const.tile([P, U], BF16, name="grow")
+        ones = const.tile([P, P], BF16, name="ones")
         ident = const.tile([P, P], F32, name="ident")
+        warm = const.tile([P, 1], F32, name="warm")
         make_identity(nc, ident[:])
+        nc.gpsimd.memset(grow[:], 0.0)
+        nc.gpsimd.memset(ones[:], 1.0)
+        nc.vector.memset(warm[:], 0.0)
+        nc.scalar.activation(out=warm[:], in_=warm[:], func=ACT.Exp)
 
-        gabs = const.tile([P, U], F32, name="gabs")
-        nc.vector.scalar_tensor_tensor(
-            out=gabs[:], in0=graw[:], scalar=-1.0, in1=graw[:], op0=ALU.mult, op1=ALU.max
-        )
-        gexp = const.tile([P, U], F32, name="gexp")
-        nc.scalar.activation(out=gexp[:], in_=gabs[:], func=ACT.Exp, scale=-1.0)
+        load(0)
+        nc.sync.dma_start(out=c_sb[:], in_=centers)
+        nc.sync.dma_start(out=grow[0:1, :], in_=gamma_raw.unsqueeze(0))
+        for g in range(1, NX):
+            load(g)
 
+        norms(0)
+        transposes(0)
+        copies(0)
         c_xt = transpose_tile(c_sb[:])
         c_grp = const.tile([P, 2, P, 2], F32, name="c_grp", align_bytes=64)
         nc.vector.tensor_copy(
@@ -208,9 +227,14 @@ def tile_rbflayer_t_kernel(tc, x, centers, gamma_raw, out):
         cn = const.tile([P, 1], F32, name="cn")
         nc.scalar.activation(out=c_junk[:], in_=c_sb[:], func=ACT.Square, accum_out=cn[:])
 
-        norms(0)
-        transposes(0)
-        copies(0)
+        g_ps = ps_r.tile([P, P], F32, name="r")
+        nc.tensor.matmul(out=g_ps[:], lhsT=ones[:], rhs=grow[:], start=True, stop=True)
+        transposes(1)
+        if 0 in V_NORM_GROUPS:
+            vnorm(0)
+        quant(0)
+        graw = const.tile([P, U], F32, name="graw")
+        nc.vector.tensor_copy(out=graw[:], in_=g_ps[:])
         c_cod = const.tile([P, 2 * P], U32, name="c_cod", align_bytes=64)
         c_scl = const.tile([P, 2 * P], U8, name="c_scl", align_bytes=64)
         nc.vector.quantize_mx(
@@ -218,49 +242,68 @@ def tile_rbflayer_t_kernel(tc, x, centers, gamma_raw, out):
             scales=c_scl[:],
             in_=c_grp[:].rearrange("p g c u -> p (g c u)").bitcast(BF16),
         )
-        transposes(1)
+        gabs = const.tile([P, U], F32, name="gabs")
+        nc.vector.scalar_tensor_tensor(
+            out=gabs[:], in0=graw[:], scalar=-1.0, in1=graw[:], op0=ALU.mult, op1=ALU.max
+        )
+        gexp = const.tile([P, U], F32, name="gexp")
+        nc.scalar.activation(out=gexp[:], in_=gabs[:], func=ACT.Exp, scale=-1.0)
         glog = const.tile([P, U], F32, name="glog")
         nc.scalar.activation(out=glog[:], in_=gexp[:], func=ACT.Ln, bias=1.0, scale=1.0)
         norms(1)
-
+        mx(0)
+        copies(1)
+        transposes(2)
+        if 1 in PE_NORM_GROUPS:
+            gram(1)
         cnh = const.tile([P, 1], F32, name="cnh")
         nc.vector.tensor_scalar(
             out=cnh[:], in0=cn[:], scalar1=EPS, scalar2=0.5, op0=ALU.add, op1=ALU.mult
         )
-        quant(0)
+        if 1 in V_NORM_GROUPS:
+            vnorm(1)
         cn_rep = const.tile([P, P], F32, name="cn_rep")
         nc.vector.tensor_copy(out=cn_rep[:], in_=cnh[:, 0:1].to_broadcast([P, P]))
-        cn_ps = ps_r.tile([P, P], F32, name="r")
+        quant(1)
+        cn_ps = ps_c.tile([P, P], F32, name="cn_ps")
         nc.tensor.transpose(cn_ps[:], cn_rep[:], ident[:])
-        gam = const.tile([P, U], F32, name="gam")
-        nc.vector.scalar_tensor_tensor(
-            out=gam[:], in0=graw[:], scalar=0.0, in1=glog[:], op0=ALU.max, op1=ALU.add
-        )
         cnb = const.tile([P, U], F32, name="cnb")
-        nc.vector.tensor_copy(out=cnb[:], in_=cn_ps[:])
+        gam = const.tile([P, U], F32, name="gam")
         g2 = const.tile([P, T, U], F32, name="g2")
-        for j in range(T):
-            nc.vector.tensor_scalar_mul(out=g2[:, j, :], in0=gam[:], scalar1=2.0)
+
+        def finish_constants():
+            nc.vector.tensor_copy(out=cnb[:], in_=cn_ps[:])
+            nc.vector.scalar_tensor_tensor(
+                out=gam[:], in0=graw[:], scalar=0.0, in1=glog[:], op0=ALU.max, op1=ALU.add
+            )
+            for j in range(T):
+                nc.vector.tensor_scalar_mul(out=g2[:, j, :], in0=gam[:], scalar1=2.0)
 
         for i in range(NG):
-            mx(i)
-            halves(i)
             if i + 1 < NG:
-                copies(i + 1)
+                mx(i + 1)
+            halves(i)
             if i + 2 < NG:
-                transposes(i + 2)
-            if i + 1 in PE_NORM_GROUPS:
-                gram(i + 1)
-            if i >= 1:
-                epi3(i - 1)
-                store(i - 1)
+                copies(i + 2)
+            if i == 0:
+                finish_constants()
+            if i + 3 < NG:
+                transposes(i + 3)
+            if i + 2 in PE_NORM_GROUPS:
+                gram(i + 2)
+            if i >= 2:
+                epi3(i - 2)
+                store(i - 2)
             if i + 2 < NG:
                 norms(i + 2)
             if i + NX < NG:
                 load(i + NX)
             epi1(i)
-            if i + 1 < NG:
-                quant(i + 1)
+            if i + 2 < NG:
+                quant(i + 2)
             epi2(i)
-        epi3(NG - 1)
-        store(NG - 1)
+            if i + 2 in V_NORM_GROUPS:
+                vnorm(i + 2)
+        for g in (NG - 2, NG - 1):
+            epi3(g)
+            store(g)

@@ -1,3 +1,4 @@
+import math
 from contextlib import ExitStack
 
 import concourse.mybir as mybir
@@ -18,6 +19,7 @@ T = 4
 NG = NT // T
 LAST = T - 1
 EPS = 1e-12
+ROOT_HALF = math.sqrt(0.5)
 NX = 6
 PE_NORM_GROUPS = (1, 4, 6, 9, 12, 14, 17, 20, 22)
 S_COPY_GROUPS = ()
@@ -72,8 +74,10 @@ def tile_rbflayer_t_kernel(tc, x, centers, gamma_raw, out):
 
         def norms(g):
             xn = small.tile([P, T], F32, name="xn")
-            xh = small.tile([P, T], F32, name="xh")
-            xns[g] = (xn, xh)
+            xo = None
+            if g in PE_NORM_GROUPS or g in V_NORM_GROUPS:
+                xo = small.tile([P, 1], F32, name="xo")
+            xns[g] = (xn, xo)
             for j in range(T):
                 if j == LAST and (g in PE_NORM_GROUPS or g in V_NORM_GROUPS):
                     continue
@@ -82,6 +86,7 @@ def tile_rbflayer_t_kernel(tc, x, centers, gamma_raw, out):
                     out=sj[:],
                     in_=x_sb[g][:, j, :],
                     func=ACT.Square,
+                    scale=ROOT_HALF,
                     accum_out=xn[:, j : j + 1],
                 )
 
@@ -90,11 +95,11 @@ def tile_rbflayer_t_kernel(tc, x, centers, gamma_raw, out):
             nc.vector.scalar_tensor_tensor(
                 out=vj[:],
                 in0=x_sb[g][:, LAST, :],
-                scalar=-0.5,
+                scalar=0.5,
                 in1=x_sb[g][:, LAST, :],
                 op0=ALU.mult,
                 op1=ALU.mult,
-                accum_out=xns[g][1][:, LAST : LAST + 1],
+                accum_out=xns[g][1][:],
             )
 
         def transposes(g):
@@ -149,34 +154,32 @@ def tile_rbflayer_t_kernel(tc, x, centers, gamma_raw, out):
                     )
 
         def halves(g):
-            xn, xh = xns[g]
-            n_s = T
-            if g in PE_NORM_GROUPS or g in V_NORM_GROUPS:
-                n_s = LAST
-            nc.vector.tensor_scalar_mul(out=xh[:, 0:n_s], in0=xn[:, 0:n_s], scalar1=-0.5)
             if g in PE_NORM_GROUPS:
                 rj = work.tile([P, P], F32, name="rj")
                 nc.vector.scalar_tensor_tensor(
                     out=rj[:],
                     in0=rps[g][:],
-                    scalar=-0.5,
+                    scalar=0.5,
                     in1=ident[:],
                     op0=ALU.mult,
                     op1=ALU.mult,
-                    accum_out=xh[:, LAST : LAST + 1],
+                    accum_out=xns[g][1][:],
                 )
 
         def epi1(g):
-            xh = xns[g][1]
+            xn, xo = xns[g]
             e = epi.tile([P, T, U], F32, name="e")
             eps_t[g] = e
             for j in range(T):
+                half_norm = xn[:, j : j + 1]
+                if j == LAST and (g in PE_NORM_GROUPS or g in V_NORM_GROUPS):
+                    half_norm = xo[:]
                 nc.vector.scalar_tensor_tensor(
                     out=e[:, j, :],
                     in0=accs[g][:, j, :],
-                    scalar=xh[:, j : j + 1],
+                    scalar=half_norm,
                     in1=cnb[:],
-                    op0=ALU.add,
+                    op0=ALU.subtract,
                     op1=ALU.subtract,
                 )
 
@@ -246,11 +249,11 @@ def tile_rbflayer_t_kernel(tc, x, centers, gamma_raw, out):
         nc.vector.scalar_tensor_tensor(
             out=gabs[:], in0=graw[:], scalar=-1.0, in1=graw[:], op0=ALU.mult, op1=ALU.max
         )
+        norms(1)
         gexp = const.tile([P, U], F32, name="gexp")
         nc.scalar.activation(out=gexp[:], in_=gabs[:], func=ACT.Exp, scale=-1.0)
         glog = const.tile([P, U], F32, name="glog")
         nc.scalar.activation(out=glog[:], in_=gexp[:], func=ACT.Ln, bias=1.0, scale=1.0)
-        norms(1)
         mx(0)
         copies(1)
         transposes(2)

@@ -23,7 +23,7 @@ ROOT_HALF = math.sqrt(0.5)
 NX = 6
 PE_NORM_GROUPS = (1, 4, 6, 9, 12, 14, 17, 20, 22)
 S_COPY_GROUPS = ()
-V_NORM_GROUPS = (0, 2)
+V_NORM_GROUPS = ()
 
 FLOPS = 2 * B * D * U
 

@@ -22,8 +22,8 @@ EPS = 1e-12
 ROOT_HALF = math.sqrt(0.5)
 NX = 6
 PE_NORM_GROUPS = (1, 4, 6, 9, 12, 14, 17, 20, 22)
-S_COPY_GROUPS = ()
-V_NORM_GROUPS = ()
+FIRST = 0
+S_COPY = 1
 
 FLOPS = 2 * B * D * U
 
@@ -39,10 +39,11 @@ def tile_rbflayer_t_kernel(tc, x, centers, gamma_raw, out):
         xin = ctx.enter_context(tc.tile_pool(name="xin", bufs=NX))
         work = ctx.enter_context(tc.tile_pool(name="work", bufs=2))
         codes = ctx.enter_context(tc.tile_pool(name="codes", bufs=3))
-        small = ctx.enter_context(tc.tile_pool(name="small", bufs=5))
+        sqp = ctx.enter_context(tc.tile_pool(name="sqp", bufs=2))
+        small = ctx.enter_context(tc.tile_pool(name="small", bufs=6))
         epi = ctx.enter_context(tc.tile_pool(name="epi", bufs=5))
         ps_t = ctx.enter_context(tc.psum_pool(name="ps_t", bufs=4))
-        ps_c = ctx.enter_context(tc.psum_pool(name="ps_c", bufs=1))
+        ps_g = ctx.enter_context(tc.psum_pool(name="ps_g", bufs=1))
         ps_r = ctx.enter_context(tc.psum_pool(name="ps_r", bufs=1))
         ps_a = ctx.enter_context(tc.psum_pool(name="ps_a", bufs=2))
 
@@ -55,6 +56,7 @@ def tile_rbflayer_t_kernel(tc, x, centers, gamma_raw, out):
         xns = {}
         eps_t = {}
         rps = {}
+        sqs = {}
 
         def load(g):
             t = xin.tile([P, T, D], BF16, name="x_sb")
@@ -74,12 +76,11 @@ def tile_rbflayer_t_kernel(tc, x, centers, gamma_raw, out):
 
         def norms(g):
             xn = small.tile([P, T], F32, name="xn")
-            xo = None
-            if g in PE_NORM_GROUPS or g in V_NORM_GROUPS:
-                xo = small.tile([P, 1], F32, name="xo")
-            xns[g] = (xn, xo)
+            xg = small.tile([P, 1], F32, name="xg")
+            xo = small.tile([P, 1], F32, name="xo") if g in PE_NORM_GROUPS else None
+            xns[g] = (xn, xg, xo)
             for j in range(T):
-                if j == LAST and (g in PE_NORM_GROUPS or g in V_NORM_GROUPS):
+                if j == FIRST or (j == LAST and g in PE_NORM_GROUPS):
                     continue
                 sj = work.tile([P, D], BF16, name="sjunk")
                 nc.scalar.activation(
@@ -90,39 +91,43 @@ def tile_rbflayer_t_kernel(tc, x, centers, gamma_raw, out):
                     accum_out=xn[:, j : j + 1],
                 )
 
-        def vnorm(g):
-            vj = work.tile([P, D], BF16, name="vjunk")
-            nc.vector.scalar_tensor_tensor(
-                out=vj[:],
-                in0=x_sb[g][:, LAST, :],
-                scalar=0.5,
-                in1=x_sb[g][:, LAST, :],
-                op0=ALU.mult,
-                op1=ALU.mult,
-                accum_out=xns[g][1][:],
-            )
-
         def transposes(g):
             xts[g] = [transpose_tile(x_sb[g][:, j, :]) for j in range(T)]
 
-        def copies(g):
-            grp = work.tile([P, T, 2, P, 2], F32, name="grp", align_bytes=64)
-            grps[g] = grp
-            for j in range(T):
-                src = xts[g][j][:].rearrange("p (g u) c -> p g c u", u=2)
-                if j == 0 and g in S_COPY_GROUPS:
-                    nc.scalar.copy(out=grp[:, j], in_=src)
-                else:
-                    nc.vector.tensor_copy(out=grp[:, j], in_=src)
+        def new_grp(g):
+            grps[g] = work.tile([P, T, 2, P, 2], F32, name="grp", align_bytes=64)
+
+        def copy_tile(g, j):
+            src = xts[g][j][:].rearrange("p (g u) c -> p g c u", u=2)
+            if j == S_COPY:
+                nc.scalar.copy(out=grps[g][:, j], in_=src)
+            else:
+                nc.vector.tensor_copy(out=grps[g][:, j], in_=src)
+
+        def squares(g):
+            sq = sqp.tile([P, 2, 4, P], F32, name="sq")
+            sqs[g] = sq
+            v = grps[g][:, FIRST].bitcast(BF16).rearrange("p g c t -> p g t c")
+            nc.gpsimd.tensor_tensor(out=sq[:], in0=v, in1=v, op=ALU.mult)
 
         def gram(g):
-            r = ps_r.tile([P, P], F32, name="r")
+            r = ps_r.tile([P, 2, P], F32, name="r")
             rps[g] = r
-            v = grps[g][:, LAST].bitcast(BF16)
+            if g in PE_NORM_GROUPS:
+                v = grps[g][:, LAST].bitcast(BF16)
+                for q in range(8):
+                    plane = v[:, q // 4, :, q % 4]
+                    nc.tensor.matmul(
+                        out=r[:, 0, :], lhsT=plane, rhs=plane, start=(q == 0), stop=(q == 7)
+                    )
             for q in range(8):
-                plane = v[:, q // 4, :, q % 4]
                 nc.tensor.matmul(
-                    out=r[:], lhsT=plane, rhs=plane, start=(q == 0), stop=(q == 7)
+                    out=r[:, 1, :],
+                    lhsT=sqs[g][:, q // 4, q % 4, :],
+                    rhs=ident[:],
+                    is_transpose=True,
+                    start=(q == 0),
+                    stop=(q == 7),
                 )
 
         def quant(g):
@@ -154,25 +159,37 @@ def tile_rbflayer_t_kernel(tc, x, centers, gamma_raw, out):
                     )
 
         def halves(g):
+            gj = work.tile([P, P], F32, name="gj")
+            nc.vector.tensor_scalar(
+                out=gj[:],
+                in0=rps[g][:, 1, :],
+                scalar1=0.5,
+                scalar2=0.0,
+                op0=ALU.mult,
+                op1=ALU.add,
+                accum_out=xns[g][1][:],
+            )
             if g in PE_NORM_GROUPS:
                 rj = work.tile([P, P], F32, name="rj")
                 nc.vector.scalar_tensor_tensor(
                     out=rj[:],
-                    in0=rps[g][:],
+                    in0=rps[g][:, 0, :],
                     scalar=0.5,
                     in1=ident[:],
                     op0=ALU.mult,
                     op1=ALU.mult,
-                    accum_out=xns[g][1][:],
+                    accum_out=xns[g][2][:],
                 )
 
         def epi1(g):
-            xn, xo = xns[g]
+            xn, xg, xo = xns[g]
             e = epi.tile([P, T, U], F32, name="e")
             eps_t[g] = e
             for j in range(T):
                 half_norm = xn[:, j : j + 1]
-                if j == LAST and (g in PE_NORM_GROUPS or g in V_NORM_GROUPS):
+                if j == FIRST:
+                    half_norm = xg[:]
+                if j == LAST and g in PE_NORM_GROUPS:
                     half_norm = xo[:]
                 nc.vector.scalar_tensor_tensor(
                     out=e[:, j, :],
@@ -189,7 +206,7 @@ def tile_rbflayer_t_kernel(tc, x, centers, gamma_raw, out):
                 out=ef,
                 in0=ef,
                 scalar=0.0,
-                in1=g2[:].rearrange("p t u -> p (t u)"),
+                in1=g2_ps[:].rearrange("p t u -> p (t u)"),
                 op0=ALU.min,
                 op1=ALU.mult,
             )
@@ -220,7 +237,10 @@ def tile_rbflayer_t_kernel(tc, x, centers, gamma_raw, out):
 
         norms(0)
         transposes(0)
-        copies(0)
+        new_grp(0)
+        for j in range(T):
+            copy_tile(0, j)
+        squares(0)
         c_xt = transpose_tile(c_sb[:])
         c_grp = const.tile([P, 2, P, 2], F32, name="c_grp", align_bytes=64)
         nc.vector.tensor_copy(
@@ -230,14 +250,14 @@ def tile_rbflayer_t_kernel(tc, x, centers, gamma_raw, out):
         cn = const.tile([P, 1], F32, name="cn")
         nc.scalar.activation(out=c_junk[:], in_=c_sb[:], func=ACT.Square, accum_out=cn[:])
 
-        g_ps = ps_r.tile([P, P], F32, name="r")
-        nc.tensor.matmul(out=g_ps[:], lhsT=ones[:], rhs=grow[:], start=True, stop=True)
+        g_ps = ps_r.tile([P, 2, P], F32, name="r")
+        nc.tensor.matmul(
+            out=g_ps[:, 0, :], lhsT=grow[:], rhs=ones[:], start=True, stop=True
+        )
         transposes(1)
-        if 0 in V_NORM_GROUPS:
-            vnorm(0)
         quant(0)
-        graw = const.tile([P, U], F32, name="graw")
-        nc.vector.tensor_copy(out=graw[:], in_=g_ps[:])
+        graw = const.tile([P, 1], F32, name="graw")
+        nc.vector.tensor_copy(out=graw[:], in_=g_ps[:, 0, 0:1])
         c_cod = const.tile([P, 2 * P], U32, name="c_cod", align_bytes=64)
         c_scl = const.tile([P, 2 * P], U8, name="c_scl", align_bytes=64)
         nc.vector.quantize_mx(
@@ -245,68 +265,80 @@ def tile_rbflayer_t_kernel(tc, x, centers, gamma_raw, out):
             scales=c_scl[:],
             in_=c_grp[:].rearrange("p g c u -> p (g c u)").bitcast(BF16),
         )
-        gabs = const.tile([P, U], F32, name="gabs")
+        gabs = const.tile([P, 1], F32, name="gabs")
         nc.vector.scalar_tensor_tensor(
             out=gabs[:], in0=graw[:], scalar=-1.0, in1=graw[:], op0=ALU.mult, op1=ALU.max
         )
+        new_grp(1)
+        copy_tile(1, S_COPY)
         norms(1)
-        gexp = const.tile([P, U], F32, name="gexp")
+        gexp = const.tile([P, 1], F32, name="gexp")
         nc.scalar.activation(out=gexp[:], in_=gabs[:], func=ACT.Exp, scale=-1.0)
-        glog = const.tile([P, U], F32, name="glog")
+        glog = const.tile([P, 1], F32, name="glog")
         nc.scalar.activation(out=glog[:], in_=gexp[:], func=ACT.Ln, bias=1.0, scale=1.0)
+        for j in range(T):
+            if j != S_COPY:
+                copy_tile(1, j)
+            if j == FIRST:
+                squares(1)
         mx(0)
-        copies(1)
+        gram(0)
         transposes(2)
-        if 1 in PE_NORM_GROUPS:
-            gram(1)
         cnh = const.tile([P, 1], F32, name="cnh")
         nc.vector.tensor_scalar(
             out=cnh[:], in0=cn[:], scalar1=EPS, scalar2=0.5, op0=ALU.add, op1=ALU.mult
         )
-        if 1 in V_NORM_GROUPS:
-            vnorm(1)
         cn_rep = const.tile([P, P], F32, name="cn_rep")
         nc.vector.tensor_copy(out=cn_rep[:], in_=cnh[:, 0:1].to_broadcast([P, P]))
         quant(1)
-        cn_ps = ps_c.tile([P, P], F32, name="cn_ps")
-        nc.tensor.transpose(cn_ps[:], cn_rep[:], ident[:])
+        halves(0)
+        gam = const.tile([P, 1], F32, name="gam")
+        nc.vector.scalar_tensor_tensor(
+            out=gam[:], in0=graw[:], scalar=0.0, in1=glog[:], op0=ALU.max, op1=ALU.add
+        )
+        cn_ps = ps_r.tile([P, 2, P], F32, name="r")
+        nc.tensor.transpose(cn_ps[:, 0, :], cn_rep[:], ident[:])
         cnb = const.tile([P, U], F32, name="cnb")
-        gam = const.tile([P, U], F32, name="gam")
-        g2 = const.tile([P, T, U], F32, name="g2")
-
-        def finish_constants():
-            nc.vector.tensor_copy(out=cnb[:], in_=cn_ps[:])
-            nc.vector.scalar_tensor_tensor(
-                out=gam[:], in0=graw[:], scalar=0.0, in1=glog[:], op0=ALU.max, op1=ALU.add
-            )
-            for j in range(T):
-                nc.vector.tensor_scalar_mul(out=g2[:, j, :], in0=gam[:], scalar1=2.0)
+        nc.vector.tensor_copy(out=cnb[:], in_=cn_ps[:, 0, :])
+        g_rep = const.tile([P, P], F32, name="g_rep")
+        nc.vector.tensor_scalar_mul(
+            out=g_rep[:], in0=gam[:, 0:1].to_broadcast([P, P]), scalar1=2.0
+        )
+        g2_ps = ps_g.tile([P, T, U], F32, name="g2_ps")
+        for j in range(T):
+            nc.tensor.transpose(g2_ps[:, j, :], g_rep[:], ident[:])
+        gram(1)
 
         for i in range(NG):
+            nxt = i + 2
             if i + 1 < NG:
                 mx(i + 1)
-            halves(i)
-            if i + 2 < NG:
-                copies(i + 2)
-            if i == 0:
-                finish_constants()
+            if nxt < NG:
+                new_grp(nxt)
+                copy_tile(nxt, FIRST)
+                squares(nxt)
+                copy_tile(nxt, S_COPY)
+            if i >= 1:
+                epi2(i - 1)
+            if i + 1 < NG:
+                halves(i + 1)
+            if nxt < NG:
+                for j in range(T):
+                    if j not in (FIRST, S_COPY):
+                        copy_tile(nxt, j)
             if i + 3 < NG:
                 transposes(i + 3)
-            if i + 2 in PE_NORM_GROUPS:
-                gram(i + 2)
-            if i >= 2:
-                epi3(i - 2)
-                store(i - 2)
-            if i + 2 < NG:
-                norms(i + 2)
+            if nxt < NG:
+                gram(nxt)
+                norms(nxt)
+            if i >= 1:
+                epi3(i - 1)
+                store(i - 1)
             if i + NX < NG:
                 load(i + NX)
             epi1(i)
-            if i + 2 < NG:
-                quant(i + 2)
-            epi2(i)
-            if i + 2 in V_NORM_GROUPS:
-                vnorm(i + 2)
-        for g in (NG - 2, NG - 1):
-            epi3(g)
-            store(g)
+            if nxt < NG:
+                quant(nxt)
+        epi2(NG - 1)
+        epi3(NG - 1)
+        store(NG - 1)

@@ -309,25 +309,24 @@ def tile_rbflayer_t_kernel(tc, x, centers, gamma_raw, out):
             nc.tensor.transpose(g2_ps[:, j, :], g_rep[:], ident[:])
         gram(1)
 
+        new_grp(2)
+        copy_tile(2, FIRST)
+        squares(2)
+
         for i in range(NG):
             nxt = i + 2
             if i + 1 < NG:
                 mx(i + 1)
             if nxt < NG:
-                new_grp(nxt)
-                copy_tile(nxt, FIRST)
-                squares(nxt)
-                copy_tile(nxt, S_COPY)
+                for j in range(T):
+                    if j != FIRST:
+                        copy_tile(nxt, j)
+            if i + 3 < NG:
+                transposes(i + 3)
             if i >= 1:
                 epi2(i - 1)
             if i + 1 < NG:
                 halves(i + 1)
-            if nxt < NG:
-                for j in range(T):
-                    if j not in (FIRST, S_COPY):
-                        copy_tile(nxt, j)
-            if i + 3 < NG:
-                transposes(i + 3)
             if nxt < NG:
                 gram(nxt)
                 norms(nxt)
@@ -337,6 +336,10 @@ def tile_rbflayer_t_kernel(tc, x, centers, gamma_raw, out):
             if i + NX < NG:
                 load(i + NX)
             epi1(i)
+            if i + 3 < NG:
+                new_grp(i + 3)
+                copy_tile(i + 3, FIRST)
+                squares(i + 3)
             if nxt < NG:
                 quant(nxt)
         epi2(NG - 1)

@@ -11,6 +11,7 @@ U8 = mybir.dt.uint8
 FP8X4 = mybir.dt.float8_e4m3fn_x4
 ALU = mybir.AluOpType
 ACT = mybir.ActivationFunctionType
+AX = mybir.AxisListType
 
 P = 128
 B, D, U = 12288, 1024, 128
@@ -23,7 +24,10 @@ ROOT_HALF = math.sqrt(0.5)
 NX = 6
 PE_NORM_GROUPS = (1, 4, 6, 9, 12, 14, 17, 20, 22)
 FIRST = 0
-S_COPY = 1
+S_COPY = (1,)
+S_COPY_END = (1, 2)
+END = NG - 3
+ALL = range(T)
 
 FLOPS = 2 * B * D * U
 
@@ -97,9 +101,12 @@ def tile_rbflayer_t_kernel(tc, x, centers, gamma_raw, out):
         def new_grp(g):
             grps[g] = work.tile([P, T, 2, P, 2], F32, name="grp", align_bytes=64)
 
+        def s_copies(g):
+            return S_COPY_END if g >= END else S_COPY
+
         def copy_tile(g, j):
             src = xts[g][j][:].rearrange("p (g u) c -> p g c u", u=2)
-            if j == S_COPY:
+            if j in s_copies(g):
                 nc.scalar.copy(out=grps[g][:, j], in_=src)
             else:
                 nc.vector.tensor_copy(out=grps[g][:, j], in_=src)
@@ -145,7 +152,8 @@ def tile_rbflayer_t_kernel(tc, x, centers, gamma_raw, out):
             acc = ps_a.tile([P, T, U], F32, name="acc")
             accs[g] = acc
             for j in range(T):
-                for h in range(2):
+                passes = (0, 1, 0, 1) if j == FIRST else (0, 1)
+                for n, h in enumerate(passes):
                     cols = slice((2 * j + h) * P, (2 * j + h + 1) * P)
                     ccols = slice(h * P, (h + 1) * P)
                     nc.tensor.matmul_mx(
@@ -154,20 +162,13 @@ def tile_rbflayer_t_kernel(tc, x, centers, gamma_raw, out):
                         lhsT_scale=scls[g][:, cols],
                         rhs=c_cod[:, ccols].bitcast(FP8X4),
                         rhs_scale=c_scl[:, ccols],
-                        start=(h == 0),
-                        stop=(h == 1),
+                        start=(n == 0),
+                        stop=(n == len(passes) - 1),
                     )
 
         def halves(g):
-            gj = work.tile([P, P], F32, name="gj")
-            nc.vector.tensor_scalar(
-                out=gj[:],
-                in0=rps[g][:, 1, :],
-                scalar1=0.5,
-                scalar2=0.0,
-                op0=ALU.mult,
-                op1=ALU.add,
-                accum_out=xns[g][1][:],
+            nc.vector.tensor_reduce(
+                out=xns[g][1][:], in_=rps[g][:, 1, :], axis=AX.X, op=ALU.add
             )
             if g in PE_NORM_GROUPS:
                 rj = work.tile([P, P], F32, name="rj")
@@ -181,42 +182,46 @@ def tile_rbflayer_t_kernel(tc, x, centers, gamma_raw, out):
                     accum_out=xns[g][2][:],
                 )
 
-        def epi1(g):
+        def epi1(g, tiles):
             xn, xg, xo = xns[g]
-            e = epi.tile([P, T, U], F32, name="e")
-            eps_t[g] = e
-            for j in range(T):
+            for j in tiles:
                 half_norm = xn[:, j : j + 1]
                 if j == FIRST:
                     half_norm = xg[:]
                 if j == LAST and g in PE_NORM_GROUPS:
                     half_norm = xo[:]
                 nc.vector.scalar_tensor_tensor(
-                    out=e[:, j, :],
+                    out=eps_t[g][:, j, :],
                     in0=accs[g][:, j, :],
                     scalar=half_norm,
-                    in1=cnb[:],
+                    in1=cnf[:] if j == FIRST else cnb[:],
                     op0=ALU.subtract,
                     op1=ALU.subtract,
                 )
 
-        def epi2(g):
-            ef = eps_t[g][:].rearrange("p t u -> p (t u)")
+        def part(t, tiles):
+            return t[:, tiles.start : tiles.stop, :].rearrange("p t u -> p (t u)")
+
+        def epi2(g, tiles):
+            ef = part(eps_t[g], tiles)
             nc.vector.scalar_tensor_tensor(
                 out=ef,
                 in0=ef,
                 scalar=0.0,
-                in1=g2_ps[:].rearrange("p t u -> p (t u)"),
+                in1=part(g2_ps, tiles),
                 op0=ALU.min,
                 op1=ALU.mult,
             )
 
-        def epi3(g):
-            ef = eps_t[g][:].rearrange("p t u -> p (t u)")
+        def epi3(g, tiles):
+            ef = part(eps_t[g], tiles)
             nc.scalar.activation(out=ef, in_=ef, func=ACT.Exp)
 
-        def store(g):
-            nc.sync.dma_start(out=ov[:, g * T : (g + 1) * T, :], in_=eps_t[g][:])
+        def store(g, tiles):
+            nc.sync.dma_start(
+                out=ov[:, g * T + tiles.start : g * T + tiles.stop, :],
+                in_=eps_t[g][:, tiles.start : tiles.stop, :],
+            )
 
         c_sb = const.tile([P, D], BF16, name="c_sb")
         grow = const.tile([P, U], BF16, name="grow")
@@ -270,26 +275,25 @@ def tile_rbflayer_t_kernel(tc, x, centers, gamma_raw, out):
             out=gabs[:], in0=graw[:], scalar=-1.0, in1=graw[:], op0=ALU.mult, op1=ALU.max
         )
         new_grp(1)
-        copy_tile(1, S_COPY)
+        for j in S_COPY:
+            copy_tile(1, j)
         norms(1)
         gexp = const.tile([P, 1], F32, name="gexp")
         nc.scalar.activation(out=gexp[:], in_=gabs[:], func=ACT.Exp, scale=-1.0)
         glog = const.tile([P, 1], F32, name="glog")
         nc.scalar.activation(out=glog[:], in_=gexp[:], func=ACT.Ln, bias=1.0, scale=1.0)
         for j in range(T):
-            if j != S_COPY:
+            if j not in S_COPY:
                 copy_tile(1, j)
             if j == FIRST:
                 squares(1)
         mx(0)
         gram(0)
         transposes(2)
-        cnh = const.tile([P, 1], F32, name="cnh")
-        nc.vector.tensor_scalar(
-            out=cnh[:], in0=cn[:], scalar1=EPS, scalar2=0.5, op0=ALU.add, op1=ALU.mult
-        )
         cn_rep = const.tile([P, P], F32, name="cn_rep")
-        nc.vector.tensor_copy(out=cn_rep[:], in_=cnh[:, 0:1].to_broadcast([P, P]))
+        nc.vector.tensor_scalar_add(
+            out=cn_rep[:], in0=cn[:, 0:1].to_broadcast([P, P]), scalar1=EPS
+        )
         quant(1)
         halves(0)
         gam = const.tile([P, 1], F32, name="gam")
@@ -299,14 +303,19 @@ def tile_rbflayer_t_kernel(tc, x, centers, gamma_raw, out):
         cn_ps = ps_r.tile([P, 2, P], F32, name="r")
         nc.tensor.transpose(cn_ps[:, 0, :], cn_rep[:], ident[:])
         cnb = const.tile([P, U], F32, name="cnb")
-        nc.vector.tensor_copy(out=cnb[:], in_=cn_ps[:, 0, :])
+        nc.vector.tensor_scalar_mul(out=cnb[:], in0=cn_ps[:, 0, :], scalar1=0.5)
+        cnf = const.tile([P, U], F32, name="cnf")
+        nc.vector.tensor_copy(out=cnf[:], in_=cn_ps[:, 0, :])
         g_rep = const.tile([P, P], F32, name="g_rep")
+        nc.vector.tensor_copy(out=g_rep[:], in_=gam[:, 0:1].to_broadcast([P, P]))
+        gg_rep = const.tile([P, P], F32, name="gg_rep")
         nc.vector.tensor_scalar_mul(
-            out=g_rep[:], in0=gam[:, 0:1].to_broadcast([P, P]), scalar1=2.0
+            out=gg_rep[:], in0=gam[:, 0:1].to_broadcast([P, P]), scalar1=2.0
         )
         g2_ps = ps_g.tile([P, T, U], F32, name="g2_ps")
         for j in range(T):
-            nc.tensor.transpose(g2_ps[:, j, :], g_rep[:], ident[:])
+            rep = g_rep if j == FIRST else gg_rep
+            nc.tensor.transpose(g2_ps[:, j, :], rep[:], ident[:])
         gram(1)
 
         new_grp(2)
@@ -324,24 +333,28 @@ def tile_rbflayer_t_kernel(tc, x, centers, gamma_raw, out):
             if i + 3 < NG:
                 transposes(i + 3)
             if i >= 1:
-                epi2(i - 1)
+                epi2(i - 1, ALL)
             if i + 1 < NG:
                 halves(i + 1)
             if nxt < NG:
                 gram(nxt)
                 norms(nxt)
             if i >= 1:
-                epi3(i - 1)
-                store(i - 1)
+                epi3(i - 1, ALL)
+                store(i - 1, ALL)
             if i + NX < NG:
                 load(i + NX)
-            epi1(i)
+            eps_t[i] = epi.tile([P, T, U], F32, name="e")
+            if i + 1 < NG:
+                epi1(i, ALL)
             if i + 3 < NG:
                 new_grp(i + 3)
                 copy_tile(i + 3, FIRST)
                 squares(i + 3)
             if nxt < NG:
                 quant(nxt)
-        epi2(NG - 1)
-        epi3(NG - 1)
-        store(NG - 1)
+        for tiles in (range(0, 2), range(2, 4)):
+            epi1(NG - 1, tiles)
+            epi2(NG - 1, tiles)
+            epi3(NG - 1, tiles)
+            store(NG - 1, tiles)

@@ -21,12 +21,12 @@ NG = NT // T
 LAST = T - 1
 EPS = 1e-12
 ROOT_HALF = math.sqrt(0.5)
+TERMS = 10
 NX = 6
 PE_NORM_GROUPS = (1, 4, 6, 9, 12, 14, 17, 20, 22)
 FIRST = 0
 S_COPY = (1,)
-S_COPY_END = (1, 2)
-END = NG - 3
+S_COPY_MORE = (1, 2)
 ALL = range(T)
 
 FLOPS = 2 * B * D * U
@@ -78,13 +78,15 @@ def tile_rbflayer_t_kernel(tc, x, centers, gamma_raw, out):
                 nc.tensor.transpose(xt[:, q, :], w[:, q * P : (q + 1) * P], ident[:])
             return xt
 
-        def norms(g):
+        def new_norms(g):
             xn = small.tile([P, T], F32, name="xn")
             xg = small.tile([P, 1], F32, name="xg")
             xo = small.tile([P, 1], F32, name="xo") if g in PE_NORM_GROUPS else None
             xns[g] = (xn, xg, xo)
-            for j in range(T):
-                if j == FIRST or (j == LAST and g in PE_NORM_GROUPS):
+
+        def norms(g, tiles=range(FIRST + 1, T)):
+            for j in tiles:
+                if j == LAST and g in PE_NORM_GROUPS:
                     continue
                 sj = work.tile([P, D], BF16, name="sjunk")
                 nc.scalar.activation(
@@ -92,7 +94,7 @@ def tile_rbflayer_t_kernel(tc, x, centers, gamma_raw, out):
                     in_=x_sb[g][:, j, :],
                     func=ACT.Square,
                     scale=ROOT_HALF,
-                    accum_out=xn[:, j : j + 1],
+                    accum_out=xns[g][0][:, j : j + 1],
                 )
 
         def transposes(g):
@@ -102,7 +104,9 @@ def tile_rbflayer_t_kernel(tc, x, centers, gamma_raw, out):
             grps[g] = work.tile([P, T, 2, P, 2], F32, name="grp", align_bytes=64)
 
         def s_copies(g):
-            return S_COPY_END if g >= END else S_COPY
+            if g == 0:
+                return ()
+            return S_COPY_MORE if g in PE_NORM_GROUPS or g == NG - 1 else S_COPY
 
         def copy_tile(g, j):
             src = xts[g][j][:].rearrange("p (g u) c -> p g c u", u=2)
@@ -229,23 +233,39 @@ def tile_rbflayer_t_kernel(tc, x, centers, gamma_raw, out):
         ident = const.tile([P, P], F32, name="ident")
         warm = const.tile([P, 1], F32, name="warm")
         make_identity(nc, ident[:])
-        nc.gpsimd.memset(grow[:], 0.0)
         nc.gpsimd.memset(ones[:], 1.0)
+        nc.vector.memset(grow[:], 0.0)
         nc.vector.memset(warm[:], 0.0)
+        nc.scalar.dma_start(out=grow[0:1, :], in_=gamma_raw.unsqueeze(0))
         nc.scalar.activation(out=warm[:], in_=warm[:], func=ACT.Exp)
 
         load(0)
         nc.sync.dma_start(out=c_sb[:], in_=centers)
-        nc.sync.dma_start(out=grow[0:1, :], in_=gamma_raw.unsqueeze(0))
         for g in range(1, NX):
             load(g)
 
+        new_norms(0)
         norms(0)
         transposes(0)
         new_grp(0)
         for j in range(T):
             copy_tile(0, j)
-        squares(0)
+            if j == FIRST:
+                squares(0)
+
+        g_ps = ps_r.tile([P, 2, P], F32, name="r")
+        nc.tensor.matmul(
+            out=g_ps[:, 0, :], lhsT=grow[:], rhs=ones[:], start=True, stop=True
+        )
+        graw = const.tile([P, 1], F32, name="graw")
+        nc.vector.tensor_copy(out=graw[:], in_=g_ps[:, 0, 0:1])
+        gabs = const.tile([P, 1], F32, name="gabs")
+        nc.vector.scalar_tensor_tensor(
+            out=gabs[:], in0=graw[:], scalar=-1.0, in1=graw[:], op0=ALU.mult, op1=ALU.max
+        )
+        gexp = const.tile([P, 1], F32, name="gexp")
+        nc.scalar.activation(out=gexp[:], in_=gabs[:], func=ACT.Exp, scale=-1.0)
+
         c_xt = transpose_tile(c_sb[:])
         c_grp = const.tile([P, 2, P, 2], F32, name="c_grp", align_bytes=64)
         nc.vector.tensor_copy(
@@ -255,14 +275,39 @@ def tile_rbflayer_t_kernel(tc, x, centers, gamma_raw, out):
         cn = const.tile([P, 1], F32, name="cn")
         nc.scalar.activation(out=c_junk[:], in_=c_sb[:], func=ACT.Square, accum_out=cn[:])
 
-        g_ps = ps_r.tile([P, 2, P], F32, name="r")
-        nc.tensor.matmul(
-            out=g_ps[:, 0, :], lhsT=grow[:], rhs=ones[:], start=True, stop=True
+        gden = const.tile([P, 1], F32, name="gden")
+        nc.vector.tensor_scalar_add(out=gden[:], in0=gexp[:], scalar1=2.0)
+        ginv = const.tile([P, 1], F32, name="ginv")
+        nc.vector.reciprocal(out=ginv[:], in_=gden[:])
+        gz = const.tile([P, 1], F32, name="gz")
+        nc.gpsimd.tensor_tensor(out=gz[:], in0=gexp[:], in1=ginv[:], op=ALU.mult)
+        gw = const.tile([P, 1], F32, name="gw")
+        nc.gpsimd.tensor_tensor(out=gw[:], in0=gz[:], in1=gz[:], op=ALU.mult)
+        gser = const.tile([P, 1], F32, name="gser")
+        nc.gpsimd.tensor_scalar(
+            out=gser[:],
+            in0=gw[:],
+            scalar1=1.0 / (2 * TERMS - 1),
+            scalar2=1.0 / (2 * TERMS - 3),
+            op0=ALU.mult,
+            op1=ALU.add,
         )
+
+        def series(terms):
+            for k in terms:
+                nc.gpsimd.tensor_scalar(
+                    out=gser[:],
+                    in0=gser[:],
+                    scalar1=gw[:],
+                    scalar2=1.0 / (2 * k + 1),
+                    op0=ALU.mult,
+                    op1=ALU.add,
+                )
+
+        series(range(TERMS - 3, 2, -1))
+
         transposes(1)
         quant(0)
-        graw = const.tile([P, 1], F32, name="graw")
-        nc.vector.tensor_copy(out=graw[:], in_=g_ps[:, 0, 0:1])
         c_cod = const.tile([P, 2 * P], U32, name="c_cod", align_bytes=64)
         c_scl = const.tile([P, 2 * P], U8, name="c_scl", align_bytes=64)
         nc.vector.quantize_mx(
@@ -270,23 +315,25 @@ def tile_rbflayer_t_kernel(tc, x, centers, gamma_raw, out):
             scales=c_scl[:],
             in_=c_grp[:].rearrange("p g c u -> p (g c u)").bitcast(BF16),
         )
-        gabs = const.tile([P, 1], F32, name="gabs")
-        nc.vector.scalar_tensor_tensor(
-            out=gabs[:], in0=graw[:], scalar=-1.0, in1=graw[:], op0=ALU.mult, op1=ALU.max
-        )
         new_grp(1)
-        for j in S_COPY:
+        for j in s_copies(1):
             copy_tile(1, j)
+        new_norms(1)
         norms(1)
-        gexp = const.tile([P, 1], F32, name="gexp")
-        nc.scalar.activation(out=gexp[:], in_=gabs[:], func=ACT.Exp, scale=-1.0)
-        glog = const.tile([P, 1], F32, name="glog")
-        nc.scalar.activation(out=glog[:], in_=gexp[:], func=ACT.Ln, bias=1.0, scale=1.0)
         for j in range(T):
-            if j not in S_COPY:
+            if j not in s_copies(1):
                 copy_tile(1, j)
             if j == FIRST:
                 squares(1)
+        series(range(2, -1, -1))
+        glog = const.tile([P, 1], F32, name="glog")
+        nc.gpsimd.tensor_scalar(
+            out=glog[:], in0=gser[:], scalar1=gz[:], scalar2=2.0, op0=ALU.mult, op1=ALU.mult
+        )
+        gam = const.tile([P, 1], F32, name="gam")
+        nc.gpsimd.tensor_scalar(
+            out=gam[:], in0=graw[:], scalar1=0.0, scalar2=glog[:], op0=ALU.max, op1=ALU.add
+        )
         mx(0)
         gram(0)
         transposes(2)
@@ -296,10 +343,6 @@ def tile_rbflayer_t_kernel(tc, x, centers, gamma_raw, out):
         )
         quant(1)
         halves(0)
-        gam = const.tile([P, 1], F32, name="gam")
-        nc.vector.scalar_tensor_tensor(
-            out=gam[:], in0=graw[:], scalar=0.0, in1=glog[:], op0=ALU.max, op1=ALU.add
-        )
         cn_ps = ps_r.tile([P, 2, P], F32, name="r")
         nc.tensor.transpose(cn_ps[:, 0, :], cn_rep[:], ident[:])
         cnb = const.tile([P, U], F32, name="cnb")
@@ -307,15 +350,18 @@ def tile_rbflayer_t_kernel(tc, x, centers, gamma_raw, out):
         cnf = const.tile([P, U], F32, name="cnf")
         nc.vector.tensor_copy(out=cnf[:], in_=cn_ps[:, 0, :])
         g_rep = const.tile([P, P], F32, name="g_rep")
-        nc.vector.tensor_copy(out=g_rep[:], in_=gam[:, 0:1].to_broadcast([P, P]))
         gg_rep = const.tile([P, P], F32, name="gg_rep")
-        nc.vector.tensor_scalar_mul(
-            out=gg_rep[:], in0=gam[:, 0:1].to_broadcast([P, P]), scalar1=2.0
-        )
         g2_ps = ps_g.tile([P, T, U], F32, name="g2_ps")
-        for j in range(T):
-            rep = g_rep if j == FIRST else gg_rep
-            nc.tensor.transpose(g2_ps[:, j, :], rep[:], ident[:])
+
+        def spread_gamma():
+            nc.vector.tensor_copy(out=g_rep[:], in_=gam[:, 0:1].to_broadcast([P, P]))
+            nc.vector.tensor_scalar_mul(
+                out=gg_rep[:], in0=gam[:, 0:1].to_broadcast([P, P]), scalar1=2.0
+            )
+            for j in range(T):
+                rep = g_rep if j == FIRST else gg_rep
+                nc.tensor.transpose(g2_ps[:, j, :], rep[:], ident[:])
+
         gram(1)
 
         new_grp(2)
@@ -338,6 +384,7 @@ def tile_rbflayer_t_kernel(tc, x, centers, gamma_raw, out):
                 halves(i + 1)
             if nxt < NG:
                 gram(nxt)
+                new_norms(nxt)
                 norms(nxt)
             if i >= 1:
                 epi3(i - 1, ALL)
@@ -353,6 +400,8 @@ def tile_rbflayer_t_kernel(tc, x, centers, gamma_raw, out):
                 squares(i + 3)
             if nxt < NG:
                 quant(nxt)
+            if i == 0:
+                spread_gamma()
         for tiles in (range(0, 2), range(2, 4)):
             epi1(NG - 1, tiles)
             epi2(NG - 1, tiles)

@@ -97,8 +97,9 @@ def tile_rbflayer_t_kernel(tc, x, centers, gamma_raw, out):
                     accum_out=xns[g][0][:, j : j + 1],
                 )
 
-        def transposes(g):
-            xts[g] = [transpose_tile(x_sb[g][:, j, :]) for j in range(T)]
+        def transposes(g, tiles):
+            for j in tiles:
+                xts[g, j] = transpose_tile(x_sb[g][:, j, :])
 
         def new_grp(g):
             grps[g] = work.tile([P, T, 2, P, 2], F32, name="grp", align_bytes=64)
@@ -109,7 +110,7 @@ def tile_rbflayer_t_kernel(tc, x, centers, gamma_raw, out):
             return S_COPY_MORE if g in PE_NORM_GROUPS or g == NG - 1 else S_COPY
 
         def copy_tile(g, j):
-            src = xts[g][j][:].rearrange("p (g u) c -> p g c u", u=2)
+            src = xts[g, j][:].rearrange("p (g u) c -> p g c u", u=2)
             if j in s_copies(g):
                 nc.scalar.copy(out=grps[g][:, j], in_=src)
             else:
@@ -246,7 +247,7 @@ def tile_rbflayer_t_kernel(tc, x, centers, gamma_raw, out):
 
         new_norms(0)
         norms(0)
-        transposes(0)
+        transposes(0, ALL)
         new_grp(0)
         for j in range(T):
             copy_tile(0, j)
@@ -306,7 +307,7 @@ def tile_rbflayer_t_kernel(tc, x, centers, gamma_raw, out):
 
         series(range(TERMS - 3, 2, -1))
 
-        transposes(1)
+        transposes(1, ALL)
         quant(0)
         c_cod = const.tile([P, 2 * P], U32, name="c_cod", align_bytes=64)
         c_scl = const.tile([P, 2 * P], U8, name="c_scl", align_bytes=64)
@@ -336,7 +337,7 @@ def tile_rbflayer_t_kernel(tc, x, centers, gamma_raw, out):
         )
         mx(0)
         gram(0)
-        transposes(2)
+        transposes(2, ALL)
         cn_rep = const.tile([P, P], F32, name="cn_rep")
         nc.vector.tensor_scalar_add(
             out=cn_rep[:], in0=cn[:, 0:1].to_broadcast([P, P]), scalar1=EPS
@@ -370,6 +371,8 @@ def tile_rbflayer_t_kernel(tc, x, centers, gamma_raw, out):
 
         for i in range(NG):
             nxt = i + 2
+            if i + 3 < NG:
+                transposes(i + 3, range(FIRST, FIRST + 1))
             if i + 1 < NG:
                 mx(i + 1)
             if nxt < NG:
@@ -377,7 +380,7 @@ def tile_rbflayer_t_kernel(tc, x, centers, gamma_raw, out):
                     if j != FIRST:
                         copy_tile(nxt, j)
             if i + 3 < NG:
-                transposes(i + 3)
+                transposes(i + 3, range(FIRST + 1, T))
             if i >= 1:
                 epi2(i - 1, ALL)
             if i + 1 < NG:

import math
from contextlib import ExitStack

import concourse.mybir as mybir
from concourse.masks import make_identity

F32 = mybir.dt.float32
BF16 = mybir.dt.bfloat16
U32 = mybir.dt.uint32
U8 = mybir.dt.uint8
FP8X4 = mybir.dt.float8_e4m3fn_x4
ALU = mybir.AluOpType
ACT = mybir.ActivationFunctionType
AX = mybir.AxisListType

P = 128
B, D, U = 12288, 1024, 128
NT = B // P
T = 4
NG = NT // T
LAST = T - 1
EPS = 1e-12
ROOT_HALF = math.sqrt(0.5)
TERMS = 10
NX = 6
PE_NORM_GROUPS = (1, 4, 6, 9, 12, 14, 17, 20, 22)
FIRST = 0
S_COPY = (1,)
S_COPY_MORE = (1, 2)
ALL = range(T)

FLOPS = 2 * B * D * U


def tile_rbflayer_t_kernel(tc, x, centers, gamma_raw, out):
    nc = tc.nc
    xv = x.rearrange("(p t) k -> p t k", t=NT)
    ov = out.rearrange("(p t) u -> p t u", t=NT)

    with ExitStack() as ctx:
        ctx.enter_context(tc.manual_schedule())
        const = ctx.enter_context(tc.tile_pool(name="const", bufs=1))
        xin = ctx.enter_context(tc.tile_pool(name="xin", bufs=NX))
        work = ctx.enter_context(tc.tile_pool(name="work", bufs=2))
        codes = ctx.enter_context(tc.tile_pool(name="codes", bufs=3))
        sqp = ctx.enter_context(tc.tile_pool(name="sqp", bufs=2))
        small = ctx.enter_context(tc.tile_pool(name="small", bufs=6))
        epi = ctx.enter_context(tc.tile_pool(name="epi", bufs=5))
        ps_t = ctx.enter_context(tc.psum_pool(name="ps_t", bufs=4))
        ps_g = ctx.enter_context(tc.psum_pool(name="ps_g", bufs=1))
        ps_r = ctx.enter_context(tc.psum_pool(name="ps_r", bufs=1))
        ps_a = ctx.enter_context(tc.psum_pool(name="ps_a", bufs=2))

        x_sb = {}
        xts = {}
        grps = {}
        cods = {}
        scls = {}
        accs = {}
        xns = {}
        eps_t = {}
        rps = {}
        sqs = {}

        def load(g):
            t = xin.tile([P, T, D], BF16, name="x_sb")
            x_sb[g] = t
            if g == 0:
                for j in range(T):
                    nc.sync.dma_start(out=t[:, j, :], in_=xv[:, j, :])
            else:
                nc.sync.dma_start(out=t[:], in_=xv[:, g * T : (g + 1) * T, :])

        def transpose_tile(src_bf16):
            xt = ps_t.tile([P, 4, P], F32, name="xt")
            w = src_bf16.bitcast(F32)
            for q in range(4):
                nc.tensor.transpose(xt[:, q, :], w[:, q * P : (q + 1) * P], ident[:])
            return xt

        def new_norms(g):
            xn = small.tile([P, T], F32, name="xn")
            xg = small.tile([P, 1], F32, name="xg")
            xo = small.tile([P, 1], F32, name="xo") if g in PE_NORM_GROUPS else None
            xns[g] = (xn, xg, xo)

        def norms(g, tiles=range(FIRST + 1, T)):
            for j in tiles:
                if j == LAST and g in PE_NORM_GROUPS:
                    continue
                sj = work.tile([P, D], BF16, name="sjunk")
                nc.scalar.activation(
                    out=sj[:],
                    in_=x_sb[g][:, j, :],
                    func=ACT.Square,
                    scale=ROOT_HALF,
                    accum_out=xns[g][0][:, j : j + 1],
                )

        def transposes(g, tiles):
            for j in tiles:
                xts[g, j] = transpose_tile(x_sb[g][:, j, :])

        def new_grp(g):
            grps[g] = work.tile([P, T, 2, P, 2], F32, name="grp", align_bytes=64)

        def s_copies(g):
            if g == 0:
                return ()
            return S_COPY_MORE if g in PE_NORM_GROUPS or g == NG - 1 else S_COPY

        def copy_tile(g, j):
            src = xts[g, j][:].rearrange("p (g u) c -> p g c u", u=2)
            if j in s_copies(g):
                nc.scalar.copy(out=grps[g][:, j], in_=src)
            else:
                nc.vector.tensor_copy(out=grps[g][:, j], in_=src)

        def squares(g):
            sq = sqp.tile([P, 2, 4, P], F32, name="sq")
            sqs[g] = sq
            v = grps[g][:, FIRST].bitcast(BF16).rearrange("p g c t -> p g t c")
            nc.gpsimd.tensor_tensor(out=sq[:], in0=v, in1=v, op=ALU.mult)

        def gram(g):
            r = ps_r.tile([P, 2, P], F32, name="r")
            rps[g] = r
            if g in PE_NORM_GROUPS:
                v = grps[g][:, LAST].bitcast(BF16)
                for q in range(8):
                    plane = v[:, q // 4, :, q % 4]
                    nc.tensor.matmul(
                        out=r[:, 0, :], lhsT=plane, rhs=plane, start=(q == 0), stop=(q == 7)
                    )
            for q in range(8):
                nc.tensor.matmul(
                    out=r[:, 1, :],
                    lhsT=sqs[g][:, q // 4, q % 4, :],
                    rhs=ident[:],
                    is_transpose=True,
                    start=(q == 0),
                    stop=(q == 7),
                )

        def quant(g):
            cod = codes.tile([P, T * 2 * P], U32, name="cod", align_bytes=64)
            scl = codes.tile([P, T * 2 * P], U8, name="scl", align_bytes=64)
            cods[g] = cod
            scls[g] = scl
            nc.vector.quantize_mx(
                out=cod[:].bitcast(FP8X4),
                scales=scl[:],
                in_=grps[g][:].rearrange("p t g c u -> p (t g c u)").bitcast(BF16),
            )

        def mx(g):
            acc = ps_a.tile([P, T, U], F32, name="acc")
            accs[g] = acc
            for j in range(T):
                passes = (0, 1, 0, 1) if j == FIRST else (0, 1)
                for n, h in enumerate(passes):
                    cols = slice((2 * j + h) * P, (2 * j + h + 1) * P)
                    ccols = slice(h * P, (h + 1) * P)
                    nc.tensor.matmul_mx(
                        out=acc[:, j, :],
                        lhsT=cods[g][:, cols].bitcast(FP8X4),
                        lhsT_scale=scls[g][:, cols],
                        rhs=c_cod[:, ccols].bitcast(FP8X4),
                        rhs_scale=c_scl[:, ccols],
                        start=(n == 0),
                        stop=(n == len(passes) - 1),
                    )

        def halves(g):
            nc.vector.tensor_reduce(
                out=xns[g][1][:], in_=rps[g][:, 1, :], axis=AX.X, op=ALU.add
            )
            if g in PE_NORM_GROUPS:
                rj = work.tile([P, P], F32, name="rj")
                nc.vector.scalar_tensor_tensor(
                    out=rj[:],
                    in0=rps[g][:, 0, :],
                    scalar=0.5,
                    in1=ident[:],
                    op0=ALU.mult,
                    op1=ALU.mult,
                    accum_out=xns[g][2][:],
                )

        def epi1(g, tiles):
            xn, xg, xo = xns[g]
            for j in tiles:
                half_norm = xn[:, j : j + 1]
                if j == FIRST:
                    half_norm = xg[:]
                if j == LAST and g in PE_NORM_GROUPS:
                    half_norm = xo[:]
                nc.vector.scalar_tensor_tensor(
                    out=eps_t[g][:, j, :],
                    in0=accs[g][:, j, :],
                    scalar=half_norm,
                    in1=cnf[:] if j == FIRST else cnb[:],
                    op0=ALU.subtract,
                    op1=ALU.subtract,
                )

        def part(t, tiles):
            return t[:, tiles.start : tiles.stop, :].rearrange("p t u -> p (t u)")

        def epi2(g, tiles):
            ef = part(eps_t[g], tiles)
            nc.vector.scalar_tensor_tensor(
                out=ef,
                in0=ef,
                scalar=0.0,
                in1=part(g2_ps, tiles),
                op0=ALU.min,
                op1=ALU.mult,
            )

        def epi3(g, tiles):
            ef = part(eps_t[g], tiles)
            nc.scalar.activation(out=ef, in_=ef, func=ACT.Exp)

        def store(g, tiles):
            nc.sync.dma_start(
                out=ov[:, g * T + tiles.start : g * T + tiles.stop, :],
                in_=eps_t[g][:, tiles.start : tiles.stop, :],
            )

        c_sb = const.tile([P, D], BF16, name="c_sb")
        grow = const.tile([P, U], BF16, name="grow")
        ones = const.tile([P, P], BF16, name="ones")
        ident = const.tile([P, P], F32, name="ident")
        warm = const.tile([P, 1], F32, name="warm")
        make_identity(nc, ident[:])
        nc.gpsimd.memset(ones[:], 1.0)
        nc.vector.memset(grow[:], 0.0)
        nc.vector.memset(warm[:], 0.0)
        nc.scalar.dma_start(out=grow[0:1, :], in_=gamma_raw.unsqueeze(0))
        nc.scalar.activation(out=warm[:], in_=warm[:], func=ACT.Exp)

        load(0)
        nc.sync.dma_start(out=c_sb[:], in_=centers)
        for g in range(1, NX):
            load(g)

        new_norms(0)
        norms(0)
        transposes(0, ALL)
        new_grp(0)
        for j in range(T):
            copy_tile(0, j)
            if j == FIRST:
                squares(0)

        g_ps = ps_r.tile([P, 2, P], F32, name="r")
        nc.tensor.matmul(
            out=g_ps[:, 0, :], lhsT=grow[:], rhs=ones[:], start=True, stop=True
        )
        graw = const.tile([P, 1], F32, name="graw")
        nc.vector.tensor_copy(out=graw[:], in_=g_ps[:, 0, 0:1])
        gabs = const.tile([P, 1], F32, name="gabs")
        nc.vector.scalar_tensor_tensor(
            out=gabs[:], in0=graw[:], scalar=-1.0, in1=graw[:], op0=ALU.mult, op1=ALU.max
        )
        gexp = const.tile([P, 1], F32, name="gexp")
        nc.scalar.activation(out=gexp[:], in_=gabs[:], func=ACT.Exp, scale=-1.0)

        c_xt = transpose_tile(c_sb[:])
        c_grp = const.tile([P, 2, P, 2], F32, name="c_grp", align_bytes=64)
        nc.vector.tensor_copy(
            out=c_grp[:], in_=c_xt[:].rearrange("p (g u) c -> p g c u", u=2)
        )
        c_junk = const.tile([P, D], BF16, name="c_junk")
        cn = const.tile([P, 1], F32, name="cn")
        nc.scalar.activation(out=c_junk[:], in_=c_sb[:], func=ACT.Square, accum_out=cn[:])

        gden = const.tile([P, 1], F32, name="gden")
        nc.vector.tensor_scalar_add(out=gden[:], in0=gexp[:], scalar1=2.0)
        ginv = const.tile([P, 1], F32, name="ginv")
        nc.vector.reciprocal(out=ginv[:], in_=gden[:])
        gz = const.tile([P, 1], F32, name="gz")
        nc.gpsimd.tensor_tensor(out=gz[:], in0=gexp[:], in1=ginv[:], op=ALU.mult)
        gw = const.tile([P, 1], F32, name="gw")
        nc.gpsimd.tensor_tensor(out=gw[:], in0=gz[:], in1=gz[:], op=ALU.mult)
        gser = const.tile([P, 1], F32, name="gser")
        nc.gpsimd.tensor_scalar(
            out=gser[:],
            in0=gw[:],
            scalar1=1.0 / (2 * TERMS - 1),
            scalar2=1.0 / (2 * TERMS - 3),
            op0=ALU.mult,
            op1=ALU.add,
        )

        def series(terms):
            for k in terms:
                nc.gpsimd.tensor_scalar(
                    out=gser[:],
                    in0=gser[:],
                    scalar1=gw[:],
                    scalar2=1.0 / (2 * k + 1),
                    op0=ALU.mult,
                    op1=ALU.add,
                )

        series(range(TERMS - 3, 2, -1))

        transposes(1, ALL)
        quant(0)
        c_cod = const.tile([P, 2 * P], U32, name="c_cod", align_bytes=64)
        c_scl = const.tile([P, 2 * P], U8, name="c_scl", align_bytes=64)
        nc.vector.quantize_mx(
            out=c_cod[:].bitcast(FP8X4),
            scales=c_scl[:],
            in_=c_grp[:].rearrange("p g c u -> p (g c u)").bitcast(BF16),
        )
        new_grp(1)
        for j in s_copies(1):
            copy_tile(1, j)
        new_norms(1)
        norms(1)
        for j in range(T):
            if j not in s_copies(1):
                copy_tile(1, j)
            if j == FIRST:
                squares(1)
        series(range(2, -1, -1))
        glog = const.tile([P, 1], F32, name="glog")
        nc.gpsimd.tensor_scalar(
            out=glog[:], in0=gser[:], scalar1=gz[:], scalar2=2.0, op0=ALU.mult, op1=ALU.mult
        )
        gam = const.tile([P, 1], F32, name="gam")
        nc.gpsimd.tensor_scalar(
            out=gam[:], in0=graw[:], scalar1=0.0, scalar2=glog[:], op0=ALU.max, op1=ALU.add
        )
        mx(0)
        gram(0)
        transposes(2, ALL)
        cn_rep = const.tile([P, P], F32, name="cn_rep")
        nc.vector.tensor_scalar_add(
            out=cn_rep[:], in0=cn[:, 0:1].to_broadcast([P, P]), scalar1=EPS
        )
        quant(1)
        halves(0)
        cn_ps = ps_r.tile([P, 2, P], F32, name="r")
        nc.tensor.transpose(cn_ps[:, 0, :], cn_rep[:], ident[:])
        cnb = const.tile([P, U], F32, name="cnb")
        nc.vector.tensor_scalar_mul(out=cnb[:], in0=cn_ps[:, 0, :], scalar1=0.5)
        cnf = const.tile([P, U], F32, name="cnf")
        nc.vector.tensor_copy(out=cnf[:], in_=cn_ps[:, 0, :])
        g_rep = const.tile([P, P], F32, name="g_rep")
        gg_rep = const.tile([P, P], F32, name="gg_rep")
        g2_ps = ps_g.tile([P, T, U], F32, name="g2_ps")

        def spread_gamma():
            nc.vector.tensor_copy(out=g_rep[:], in_=gam[:, 0:1].to_broadcast([P, P]))
            nc.vector.tensor_scalar_mul(
                out=gg_rep[:], in0=gam[:, 0:1].to_broadcast([P, P]), scalar1=2.0
            )
            for j in range(T):
                rep = g_rep if j == FIRST else gg_rep
                nc.tensor.transpose(g2_ps[:, j, :], rep[:], ident[:])

        gram(1)

        new_grp(2)
        copy_tile(2, FIRST)
        squares(2)

        for i in range(NG):
            nxt = i + 2
            if i + 3 < NG:
                transposes(i + 3, range(FIRST, FIRST + 1))
            if i + 1 < NG:
                mx(i + 1)
            if nxt < NG:
                for j in range(T):
                    if j != FIRST:
                        copy_tile(nxt, j)
            if i + 3 < NG:
                transposes(i + 3, range(FIRST + 1, T))
            if i >= 1:
                epi2(i - 1, ALL)
            if i + 1 < NG:
                halves(i + 1)
            if nxt < NG:
                gram(nxt)
                new_norms(nxt)
                norms(nxt)
            if i >= 1:
                epi3(i - 1, ALL)
                store(i - 1, ALL)
            if i + NX < NG:
                load(i + NX)
            eps_t[i] = epi.tile([P, T, U], F32, name="e")
            if i + 1 < NG:
                epi1(i, ALL)
            if i + 3 < NG:
                new_grp(i + 3)
                copy_tile(i + 3, FIRST)
                squares(i + 3)
            if nxt < NG:
                quant(nxt)
            if i == 0:
                spread_gamma()
        for tiles in (range(0, 2), range(2, 4)):
            epi1(NG - 1, tiles)
            epi2(NG - 1, tiles)
            epi3(NG - 1, tiles)
            store(NG - 1, tiles)
